import numpy as np
import ml_dtypes


def mxq(x, axis, fmt="e4m3"):
    dtype, down = {"e4m3": (ml_dtypes.float8_e4m3fn, 7), "e5m2": (ml_dtypes.float8_e5m2, 14)}[fmt]
    v = np.moveaxis(np.asarray(x, np.float32).astype(ml_dtypes.bfloat16).astype(np.float64), axis, -1)
    blocks = v.reshape(v.shape[:-1] + (-1, 32))
    amax = np.abs(blocks).max(-1, keepdims=True)
    byte = np.maximum(np.where(amax > 0, np.frexp(amax)[1] - 1 + 127, 0) - down, 1)
    scale = np.exp2(byte - 127.0)
    codes = (blocks / scale).astype(np.float32).astype(dtype).astype(np.float64)
    return np.moveaxis((codes * scale).reshape(v.shape), -1, axis)


WIDE = False


def mx_kscale(k):
    if not WIDE:
        return np.ones(k)
    levels = np.array([18, -18])
    if k % 512:
        return np.exp2(np.random.permutation(np.resize(levels, k // 32))).repeat(32)
    a = np.empty((k // 512, 16))
    for p in range(k // 512):
        a[p, :8] = np.random.permutation(np.resize(levels, 8))
        for g in range(8):
            far = levels[np.abs(levels - a[p, g]) >= 10]
            a[p, g + 8] = far[np.random.randint(len(far))]
    return np.exp2(a.ravel()).repeat(32)


BF16 = ml_dtypes.bfloat16


def bf(x):
    return np.asarray(x, np.float32).astype(BF16)


def f64(x):
    return np.asarray(x).astype(np.float64)


N, C, H, W, B = 1024, 128, 4, 4, 1024
D = C * H * W
EPS = 1e-8
TINY = 1e-16


def address(mem_flat, k, strength, sharpen):
    key_norm = np.sqrt((k * k).sum(1, keepdims=True))
    mem_norm = np.sqrt((mem_flat * mem_flat).sum(1))
    sim = (k @ mem_flat.T) / (np.maximum(key_norm, EPS) * np.maximum(mem_norm, EPS)[None, :])
    z = strength * sim
    e = np.exp(z - z.max(1, keepdims=True))
    p = e / e.sum(1, keepdims=True)
    q = p ** sharpen
    return sim, q / (q.sum(1, keepdims=True) + TINY)


def setup_inputs():
    s = mx_kscale(B)[:, None]
    u = mx_kscale(N)[:, None]
    key0 = bf(np.random.standard_normal((B, D)) * (0.5 + np.random.random((B, 1))))
    mem0 = bf(np.random.standard_normal((N, D)) * (0.5 + np.random.random((N, 1))) * 3.0)
    strength = bf(np.sqrt(D) * (0.5 + 0.5 * np.random.random((B, 1))))
    sharpen = bf(1.0 + np.random.random((B, 1)))
    g = bf(np.random.standard_normal((B, N)) * np.exp2(np.random.randint(-6, 1, (B, 1))) * 16384.0)
    sim, w = address(f64(mem0), f64(key0), f64(strength), f64(sharpen))
    return {"memory": bf((f64(mem0) / u).reshape(N, C, H, W)), "key": bf(f64(key0) * s), "strength": strength, "sharpen": sharpen, "sim": np.asarray(sim, np.float32), "w": np.asarray(w, np.float32), "grad_out": g}


def reference(memory, key, strength, sharpen, sim, w, grad_out):
    mem = f64(memory).reshape(N, D)
    k = f64(key)
    wf = f64(w)
    g = f64(grad_out)
    kn = np.maximum(np.sqrt((k * k).sum(1, keepdims=True)), EPS)
    mn = np.maximum(np.sqrt((mem * mem).sum(1)), EPS)
    dsim = f64(strength) * f64(sharpen) * wf * (g - (wf * g).sum(1, keepdims=True))
    ddot = dsim / (kn * mn[None, :])
    r = dsim * f64(sim)
    dkey = mxq(ddot, 1, "e5m2") @ mxq(mem, 0, "e4m3")
    dkey = dkey - k * (r.sum(1, keepdims=True) / (kn * kn))
    dmem = mxq(ddot, 0, "e5m2").T @ mxq(k, 0, "e4m3")
    dmem = dmem - mem * (r.sum(0) / (mn * mn))[:, None]
    return dkey, dmem.reshape(N, C, H, W)

@@ -1,0 +1,397 @@
+from contextlib import ExitStack
+
+import concourse.mybir as mybir
+from concourse.masks import make_identity
+
+P = 128
+J = 4
+G = 2
+N = 1024
+D = 2048
+DC = 512
+FLOPS = 4 * 1024 * 1024 * 2048
+
+F32 = mybir.dt.float32
+BF16 = mybir.dt.bfloat16
+U32 = mybir.dt.uint32
+U8 = mybir.dt.uint8
+E4M3 = mybir.dt.float8_e4m3fn_x4
+E5M2 = mybir.dt.float8_e5m2_x4
+MULT = mybir.AluOpType.mult
+ADD = mybir.AluOpType.add
+SUB = mybir.AluOpType.subtract
+COPY = mybir.ActivationFunctionType.Copy
+SQUARE = mybir.ActivationFunctionType.Square
+
+
+def tile_memory_pa_v_kernel(tc, memory, key, strength, sharpen, sim, w, grad_out, out_0, out_1):
+    nc = tc.nc
+    mem_hbm = memory.rearrange("(g p j) c h w -> p g j (c h w)", p=P, j=J)
+    key_hbm = key.rearrange("(g p j) d -> p g j d", p=P, j=J)
+    w_hbm = w.rearrange("(g p j) n -> p g j n", p=P, j=J)
+    sim_hbm = sim.rearrange("(g p j) n -> p g j n", p=P, j=J)
+    go_hbm = grad_out.rearrange("(g p j) n -> p g j n", p=P, j=J)
+    out_0_hbm = out_0.rearrange("(g p j) d -> p g j d", p=P, j=J)
+    out_1_hbm = out_1.rearrange("(g p j) c h w -> p g j (c h w)", p=P, j=J)
+
+    with ExitStack() as ctx:
+        keep = ctx.enter_context(tc.tile_pool(name="keep", bufs=1))
+        rows = ctx.enter_context(tc.tile_pool(name="rows", bufs=8))
+        psum = ctx.enter_context(tc.psum_pool(name="psum", bufs=4))
+
+        mem_raw = keep.tile([P, G, J, D], BF16, name="mem_raw")
+        key_raw = keep.tile([P, G, J, D], BF16, name="key_raw")
+        mem_codes = keep.tile([P, G, D], U32, name="mem_codes", align_bytes=64)
+        mem_scales = keep.tile([P, G, D], U8, name="mem_scales", align_bytes=64)
+        key_codes = keep.tile([P, G, D], U32, name="key_codes", align_bytes=64)
+        key_scales = keep.tile([P, G, D], U8, name="key_scales", align_bytes=64)
+        tok_codes = keep.tile([P, G, N], U32, name="tok_codes", align_bytes=64)
+        tok_scales = keep.tile([P, G, N], U8, name="tok_scales", align_bytes=64)
+        slot_codes = keep.tile([P, G, N], U32, name="slot_codes", align_bytes=64)
+        slot_scales = keep.tile([P, G, N], U8, name="slot_scales", align_bytes=64)
+        squares = keep.tile([P, D], BF16, name="squares")
+        minv_row = keep.tile([P, N], F32, name="minv_row")
+        ident = keep.tile([P, P], F32, name="ident")
+        products = keep.tile([P, P], BF16, name="products")
+        ones = keep.tile([P, 1], F32, name="ones")
+        half = keep.tile([P, 8], F32, name="half")
+        strength_sb = keep.tile([P, G, J], BF16, name="strength_sb")
+        sharpen_sb = keep.tile([P, G, J], BF16, name="sharpen_sb")
+        fac = keep.tile([P, 8], F32, name="fac")
+        mem_ss = keep.tile([P, 8], F32, name="mem_ss")
+        key_ss = keep.tile([P, 8], F32, name="key_ss")
+        mem_inv = keep.tile([P, 8], F32, name="mem_inv")
+        key_inv = keep.tile([P, 8], F32, name="key_inv")
+        neg_c = keep.tile([P, 8], F32, name="neg_c")
+        row_sum = keep.tile([P, 8], F32, name="row_sum")
+        scl = keep.tile([P, 8], F32, name="scl")
+        neg_rk = keep.tile([P, 8], F32, name="neg_rk")
+        neg_rm = keep.tile([P, 8], F32, name="neg_rm")
+        col_sum = keep.tile([P, 8], F32, name="col_sum")
+
+        w_sb, sim_sb, go_sb, wg_sb, dd_sb, grp = {}, {}, {}, {}, {}, {}
+
+        def load_w(g, j):
+            w_sb[g, j] = rows.tile([P, N], F32, name="w_row")
+            nc.sync.dma_start(out=w_sb[g, j][:], in_=w_hbm[:, g, j, :])
+
+        def load_go(g, j):
+            go_sb[g, j] = rows.tile([P, N], BF16, name="go_row", bufs=4)
+            nc.sync.dma_start(out=go_sb[g, j][:], in_=go_hbm[:, g, j, :])
+
+        def load_sim(g, j):
+            sim_sb[g, j] = rows.tile([P, N], F32, name="sim_row", bufs=5)
+            nc.sync.dma_start(out=sim_sb[g, j][:], in_=sim_hbm[:, g, j, :])
+
+        def load_mem(g, j):
+            nc.sync.dma_start(out=mem_raw[:, g, j, :], in_=mem_hbm[:, g, j, :])
+
+        def load_key(g, j):
+            nc.sync.dma_start(out=key_raw[:, g, j, :], in_=key_hbm[:, g, j, :])
+
+        def norm(raw, ss, g, j):
+            col = 4 * g + j
+            nc.scalar.activation(out=squares[:], in_=raw[:, g, j, :], func=SQUARE, accum_out=ss[:, col : col + 1])
+
+        def gram(raw, ss, g, j):
+            words = raw[:, g, j, :].bitcast(F32)
+            turned = rows.tile([P, 8, P, 2], BF16, name="grouped", bufs=5, align_bytes=64)
+            turned_words = turned[:].rearrange("p k r e -> p (k r e)").bitcast(F32)
+            for h in range(2):
+                bank = psum.tile([P, 4, P], F32, name="flip", bufs=3)
+                for k in range(4):
+                    nc.tensor.transpose(bank[:, k, :], words[:, 128 * (4 * h + k) : 128 * (4 * h + k + 1)], ident[:])
+                nc.scalar.copy(out=turned_words[:, 512 * h : 512 * (h + 1)], in_=bank[:].rearrange("p k r -> p (k r)"))
+            acc = psum.tile([P, P], F32, name="acc")
+            for k in range(8):
+                for e in range(2):
+                    half_rows = turned[:, k, :, e]
+                    nc.tensor.matmul(acc[:], lhsT=half_rows, rhs=half_rows, start=(k == 0 and e == 0), stop=(k == 7 and e == 1))
+            col = 4 * g + j
+            nc.vector.scalar_tensor_tensor(
+                out=products[:], in0=acc[:], scalar=1.0, in1=ident[:], op0=MULT, op1=MULT, accum_out=ss[:, col : col + 1]
+            )
+
+        def inverse_norm(ss, inv, g):
+            cols = slice(4 * g, 4 * g + 4)
+            nc.vector.tensor_scalar(out=ss[:, cols], in0=ss[:, cols], scalar1=1e-16, scalar2=None, op0=mybir.AluOpType.max)
+            nc.gpsimd.tensor_tensor(out=inv[:, cols], in0=ss[:, cols], in1=half[:, cols], op=mybir.AluOpType.pow)
+
+        def spread_minv(g):
+            bank = psum.tile([P, J, P], F32, name="flip", bufs=3)
+            for j in range(J):
+                col = 4 * g + j
+                nc.tensor.transpose(bank[:, j, :], mem_inv[:, col : col + 1].to_broadcast([P, P]), ident[:])
+            nc.vector.tensor_copy(
+                out=minv_row[:, 512 * g : 512 * (g + 1)].rearrange("p (m j) -> p m j", j=J), in_=bank[:].rearrange("p j m -> p m j")
+            )
+
+        def v1(g, j):
+            col = 4 * g + j
+            wg_sb[g, j] = rows.tile([P, N], F32, name="wg_row", bufs=2)
+            nc.vector.scalar_tensor_tensor(
+                out=wg_sb[g, j][:], in0=w_sb[g, j][:], scalar=-1.0, in1=go_sb[g, j][:], op0=MULT, op1=MULT, accum_out=neg_c[:, col : col + 1]
+            )
+
+        def v2(g, j):
+            col = 4 * g + j
+            nc.vector.scalar_tensor_tensor(
+                out=w_sb[g, j][:], in0=w_sb[g, j][:], scalar=neg_c[:, col : col + 1], in1=wg_sb[g, j][:], op0=MULT, op1=SUB
+            )
+
+        def v3(g, j):
+            col = 4 * g + j
+            nc.vector.scalar_tensor_tensor(
+                out=sim_sb[g, j][:], in0=w_sb[g, j][:], scalar=fac[:, col : col + 1], in1=sim_sb[g, j][:], op0=MULT, op1=MULT,
+                accum_out=row_sum[:, col : col + 1],
+            )
+
+        def colsum(g, j):
+            for blk in range(8):
+                q, t = divmod(blk, J)
+                nc.tensor.matmul(
+                    sums[:, blk, 4 * g + j : 4 * g + j + 1], lhsT=sim_sb[g, j][:, 512 * q + t : 512 * (q + 1) : J], rhs=ones[:], start=True, stop=True
+                )
+
+        def scales_of_group(g):
+            cols = slice(4 * g, 4 * g + 4)
+            nc.vector.tensor_mul(scl[:, cols], fac[:, cols], key_inv[:, cols])
+
+        def rk_of_group(g):
+            cols = slice(4 * g, 4 * g + 4)
+            nc.vector.scalar_tensor_tensor(out=neg_rk[:, cols], in0=row_sum[:, cols], scalar=-1.0, in1=key_inv[:, cols], op0=MULT, op1=MULT)
+            nc.vector.tensor_mul(neg_rk[:, cols], neg_rk[:, cols], key_inv[:, cols])
+
+        def rm_of_all():
+            nc.vector.tensor_reduce(out=col_sum[:], in_=sums[:], axis=mybir.AxisListType.X, op=ADD)
+            nc.vector.scalar_tensor_tensor(out=neg_rm[:], in0=col_sum[:], scalar=-1.0, in1=mem_inv[:], op0=MULT, op1=MULT)
+            nc.vector.tensor_mul(neg_rm[:], neg_rm[:], mem_inv[:])
+
+        def v4(g, j):
+            col = 4 * g + j
+            if j == 0:
+                dd_sb[g] = rows.tile([P, J, N], BF16, name="dd", bufs=1)
+            nc.vector.scalar_tensor_tensor(
+                out=dd_sb[g][:, j, :], in0=w_sb[g, j][:], scalar=scl[:, col : col + 1], in1=minv_row[:], op0=MULT, op1=MULT
+            )
+
+        def ilv(raw, g, dc, eng):
+            t = rows.tile([P, DC, J], BF16, name="grouped", bufs=5, align_bytes=64)
+            grp["mem" if raw is mem_raw else "key", g, dc] = t
+            out = t[:].rearrange("p (c i) j -> p c j i", i=4)
+            in_ = raw[:, g, :, dc * DC : (dc + 1) * DC].rearrange("p j (c i) -> p c j i", i=4)
+            if eng == "S":
+                nc.scalar.copy(out=out, in_=in_)
+            elif eng == "V":
+                nc.vector.tensor_copy(out=out, in_=in_)
+            else:
+                nc.gpsimd.tensor_scalar(out=out, in0=in_, scalar1=1.0, scalar2=0.0, op0=MULT, op1=ADD)
+
+        def quant(name, g, dc):
+            codes, scales = (mem_codes, mem_scales) if name == "mem" else (key_codes, key_scales)
+            cols = slice(dc * DC, (dc + 1) * DC)
+            t = grp[name, g, dc]
+            nc.vector.quantize_mx(out=codes[:, g, cols].bitcast(E4M3), scales=scales[:, g, cols], in_=t[:].rearrange("p c j -> p (c j)"))
+
+        def tok_ilv(g, q, eng):
+            t = rows.tile([P, DC, J], BF16, name="grouped", bufs=5, align_bytes=64)
+            grp["tok", g, q] = t
+            out = t[:].rearrange("p (t m) j -> p t m j", t=J)
+            in_ = dd_sb[g][:, :, 512 * q : 512 * (q + 1)].rearrange("p j (m t) -> p t m j", t=J)
+            if eng == "V":
+                nc.vector.tensor_copy(out=out, in_=in_)
+            else:
+                nc.scalar.copy(out=out, in_=in_)
+
+        def tok_quant(g, q):
+            cols = slice(512 * q, 512 * (q + 1))
+            t = grp["tok", g, q]
+            nc.vector.quantize_mx(out=tok_codes[:, g, cols].bitcast(E5M2), scales=tok_scales[:, g, cols], in_=t[:].rearrange("p c j -> p (c j)"))
+
+        def flip(g, q):
+            words = dd_sb[g][:].rearrange("p j n -> p (j n)").bitcast(F32)
+            t = rows.tile([P, DC, J], BF16, name="grouped", bufs=5, align_bytes=64)
+            grp["slot", g, q] = t
+            t_words = t[:].rearrange("p c t -> p (c t)").bitcast(F32)
+            for jj in range(2):
+                bank = psum.tile([P, 2, 2, P], F32, name="flip", bufs=3)
+                for e in range(2):
+                    for v in range(2):
+                        first = 512 * (2 * jj + e) + 256 * q + v
+                        nc.tensor.transpose(bank[:, e, v, :], words[:, first : first + 255 : 2], ident[:])
+                nc.scalar.copy(
+                    out=t_words[:, 512 * jj : 512 * (jj + 1)].rearrange("p (e b v) -> p e b v", e=2, v=2), in_=bank[:].rearrange("p e v b -> p e b v")
+                )
+
+        def slot_quant(g, q):
+            cols = slice(512 * g, 512 * (g + 1))
+            t = grp["slot", g, q]
+            nc.vector.quantize_mx(out=slot_codes[:, q, cols].bitcast(E5M2), scales=slot_scales[:, q, cols], in_=t[:].rearrange("p c t -> p (c t)"))
+
+        accs = {}
+
+        def mm(o, g, j, dc):
+            acc = psum.tile([P, DC], F32, name="acc")
+            accs[o, g, j, dc] = acc
+            first = 512 * g + 128 * j
+            for q in range(G):
+                if o == 0:
+                    lc, ls, rc, rs = slot_codes[:, q, first : first + P], slot_scales[:, q, first : first + P], mem_codes, mem_scales
+                else:
+                    lc, ls, rc, rs = tok_codes[:, q, first : first + P], tok_scales[:, q, first : first + P], key_codes, key_scales
+                cols = slice(dc * DC, (dc + 1) * DC)
+                nc.tensor.matmul_mx(
+                    acc[:], lhsT=lc.bitcast(E5M2), lhsT_scale=ls, rhs=rc[:, q, cols].bitcast(E4M3), rhs_scale=rs[:, q, cols], start=(q == 0), stop=(q == G - 1)
+                )
+
+        stage = {}
+
+        def v5(o, g, j, dc, eng="V"):
+            if dc % 2 == 0:
+                stage[o, g, j, dc // 2] = rows.tile([P, N], F32, name="w_row")
+            col = 4 * g + j
+            raw, neg = (key_raw, neg_rk) if o == 0 else (mem_raw, neg_rm)
+            h = dc % 2
+            out = stage[o, g, j, dc // 2][:, h * DC : (h + 1) * DC]
+            r = raw[:, g, j, dc * DC : (dc + 1) * DC]
+            n = neg[:, col : col + 1]
+            acc = accs[o, g, j, dc]
+            if eng == "V":
+                nc.vector.scalar_tensor_tensor(out=out, in0=r, scalar=n, in1=acc[:], op0=MULT, op1=ADD)
+            else:
+                nc.scalar.copy(out=out, in_=acc[:])
+                y = rows.tile([P, DC], F32, name="term", bufs=2)
+                if eng == "G":
+                    nc.gpsimd.tensor_scalar(out=y[:], in0=r, scalar1=n, scalar2=0.0, op0=MULT, op1=ADD)
+                else:
+                    nc.scalar.activation(out=y[:], in_=r, func=COPY, scale=n)
+                nc.gpsimd.tensor_tensor(out=out, in0=out, in1=y[:], op=ADD)
+
+        def store(o, g, j, h):
+            hbm = out_0_hbm if o == 0 else out_1_hbm
+            nc.sync.dma_start(out=hbm[:, g, j, 2 * h * DC : 2 * (h + 1) * DC], in_=stage[o, g, j, h][:])
+
+        load_go(0, 0)
+        load_w(0, 0)
+        nc.sync.dma_start(out=strength_sb[:], in_=strength.rearrange("(g p j) o -> p g (j o)", p=P, j=J))
+        nc.sync.dma_start(out=sharpen_sb[:], in_=sharpen.rearrange("(g p j) o -> p g (j o)", p=P, j=J))
+        load_mem(0, 0)
+        load_mem(0, 1)
+        load_sim(0, 0)
+        load_mem(0, 2)
+        load_mem(0, 3)
+        load_go(0, 1)
+        load_w(0, 1)
+        load_sim(0, 1)
+        load_mem(1, 0)
+        load_go(0, 2)
+        load_w(0, 2)
+        load_mem(1, 1)
+        load_sim(0, 2)
+        load_mem(1, 2)
+        load_go(0, 3)
+        load_w(0, 3)
+        load_mem(1, 3)
+        load_sim(0, 3)
+        load_key(0, 0)
+        load_key(0, 1)
+        load_key(0, 2)
+        load_key(0, 3)
+        load_go(1, 0)
+        load_w(1, 0)
+        load_sim(1, 0)
+        load_key(1, 0)
+        load_go(1, 1)
+        load_w(1, 1)
+        load_sim(1, 1)
+        load_key(1, 1)
+        load_go(1, 2)
+        load_w(1, 2)
+        load_sim(1, 2)
+        load_key(1, 2)
+        load_go(1, 3)
+        load_w(1, 3)
+        load_sim(1, 3)
+        load_key(1, 3)
+        nc.vector.memset(half[:], -0.5)
+        nc.vector.memset(ones[:], 1.0)
+        make_identity(nc, ident[:])
+        sums = psum.tile([P, 8, 8], F32, name="sums", bufs=1)
+        nc.vector.tensor_mul(fac[:], strength_sb[:].rearrange("p g j -> p (g j)"), sharpen_sb[:].rearrange("p g j -> p (g j)"))
+
+        def elem(g, j):
+            v1(g, j)
+            v2(g, j)
+            v3(g, j)
+            colsum(g, j)
+
+        units = [(j, dc) for j in range(J) for dc in range(4)]
+
+        def out_units(o, g, items, engines):
+            for k, (j, dc) in enumerate(items):
+                mm(o, g, j, dc)
+                v5(o, g, j, dc, engines[k % len(engines)])
+                if dc % 2 == 1:
+                    store(o, g, j, dc // 2)
+
+        for j in range(J):
+            elem(0, j)
+            gram(mem_raw, mem_ss, 0, j)
+        inverse_norm(mem_ss, mem_inv, 0)
+        spread_minv(0)
+        for dc in range(4):
+            ilv(mem_raw, 0, dc, "SVSV"[dc])
+            quant("mem", 0, dc)
+        for j in range(J):
+            gram(mem_raw, mem_ss, 1, j)
+        inverse_norm(mem_ss, mem_inv, 1)
+        spread_minv(1)
+        for j in range(J):
+            gram(key_raw, key_ss, 0, j)
+        inverse_norm(key_ss, key_inv, 0)
+        scales_of_group(0)
+        for j in range(J):
+            v4(0, j)
+        rk_of_group(0)
+        for dc in range(4):
+            ilv(mem_raw, 1, dc, "SSSS"[dc])
+            quant("mem", 1, dc)
+        flip(0, 0)
+        flip(0, 1)
+        slot_quant(0, 0)
+        slot_quant(0, 1)
+        for j in range(J):
+            norm(key_raw, key_ss, 1, j)
+        inverse_norm(key_ss, key_inv, 1)
+        scales_of_group(1)
+        for j in range(J):
+            elem(1, j)
+            if j == 1:
+                for q in range(G):
+                    tok_ilv(0, q, "S")
+                    tok_quant(0, q)
+        for j in range(J):
+            v4(1, j)
+        flip(1, 0)
+        flip(1, 1)
+        slot_quant(1, 0)
+        slot_quant(1, 1)
+        rk_of_group(1)
+        out_units(0, 0, units, "V")
+        for q in range(G):
+            tok_ilv(1, q, "S")
+            tok_quant(1, q)
+        rm_of_all()
+        ilv(key_raw, 0, 0, "S")
+        ilv(key_raw, 1, 0, "S")
+        quant("key", 0, 0)
+        quant("key", 1, 0)
+        out_units(0, 1, units, "V")
+        for dc in range(1, 4):
+            ilv(key_raw, 0, dc, "S")
+            ilv(key_raw, 1, dc, "S")
+            quant("key", 0, dc)
+            quant("key", 1, dc)
+        for h in range(2):
+            for g in range(G):
+                out_units(1, g, [(j, 2 * h + e) for j in range(J) for e in range(2)], "V")

@@ -279,9 +279,9 @@ def tile_memory_pa_v_kernel(tc, memory, key, strength, sharpen, sim, w, grad_out
         load_mem(0, 1)
         load_sim(0, 0)
         load_mem(0, 2)
-        load_mem(0, 3)
         load_go(0, 1)
         load_w(0, 1)
+        load_mem(0, 3)
         load_sim(0, 1)
         load_mem(1, 0)
         load_go(0, 2)
@@ -295,24 +295,24 @@ def tile_memory_pa_v_kernel(tc, memory, key, strength, sharpen, sim, w, grad_out
         load_sim(0, 3)
         load_key(0, 0)
         load_key(0, 1)
-        load_key(0, 2)
-        load_key(0, 3)
         load_go(1, 0)
         load_w(1, 0)
+        load_key(0, 2)
         load_sim(1, 0)
-        load_key(1, 0)
+        load_key(0, 3)
         load_go(1, 1)
         load_w(1, 1)
+        load_key(1, 0)
         load_sim(1, 1)
         load_key(1, 1)
         load_go(1, 2)
         load_w(1, 2)
-        load_sim(1, 2)
         load_key(1, 2)
+        load_sim(1, 2)
+        load_key(1, 3)
         load_go(1, 3)
         load_w(1, 3)
         load_sim(1, 3)
-        load_key(1, 3)
         nc.vector.memset(half[:], -0.5)
         nc.vector.memset(ones[:], 1.0)
         make_identity(nc, ident[:])
@@ -336,62 +336,57 @@ def tile_memory_pa_v_kernel(tc, memory, key, strength, sharpen, sim, w, grad_out
 
         for j in range(J):
             elem(0, j)
-            gram(mem_raw, mem_ss, 0, j)
+            norm(mem_raw, mem_ss, 0, j)
         inverse_norm(mem_ss, mem_inv, 0)
         spread_minv(0)
-        for dc in range(4):
-            ilv(mem_raw, 0, dc, "SVSV"[dc])
-            quant("mem", 0, dc)
         for j in range(J):
-            gram(mem_raw, mem_ss, 1, j)
+            norm(mem_raw, mem_ss, 1, j)
         inverse_norm(mem_ss, mem_inv, 1)
         spread_minv(1)
         for j in range(J):
-            gram(key_raw, key_ss, 0, j)
+            norm(key_raw, key_ss, 0, j)
         inverse_norm(key_ss, key_inv, 0)
         scales_of_group(0)
         for j in range(J):
             v4(0, j)
+        for q in range(G):
+            flip(0, q)
+            slot_quant(0, q)
         rk_of_group(0)
         for dc in range(4):
+            ilv(mem_raw, 0, dc, "VVVV"[dc])
+            quant("mem", 0, dc)
             ilv(mem_raw, 1, dc, "SSSS"[dc])
             quant("mem", 1, dc)
-        flip(0, 0)
-        flip(0, 1)
-        slot_quant(0, 0)
-        slot_quant(0, 1)
         for j in range(J):
             norm(key_raw, key_ss, 1, j)
         inverse_norm(key_ss, key_inv, 1)
         scales_of_group(1)
+        for q in range(G):
+            tok_ilv(0, q, "S")
+            tok_quant(0, q)
         for j in range(J):
             elem(1, j)
-            if j == 1:
-                for q in range(G):
-                    tok_ilv(0, q, "S")
-                    tok_quant(0, q)
         for j in range(J):
             v4(1, j)
-        flip(1, 0)
-        flip(1, 1)
-        slot_quant(1, 0)
-        slot_quant(1, 1)
+        for q in range(G):
+            flip(1, q)
+            slot_quant(1, q)
         rk_of_group(1)
         out_units(0, 0, units, "V")
         for q in range(G):
             tok_ilv(1, q, "S")
             tok_quant(1, q)
         rm_of_all()
-        ilv(key_raw, 0, 0, "S")
-        ilv(key_raw, 1, 0, "S")
-        quant("key", 0, 0)
-        quant("key", 1, 0)
+        for dc in range(2):
+            for g in range(G):
+                ilv(key_raw, g, dc, "S")
+                quant("key", g, dc)
         out_units(0, 1, units, "V")
-        for dc in range(1, 4):
-            ilv(key_raw, 0, dc, "S")
-            ilv(key_raw, 1, dc, "S")
-            quant("key", 0, dc)
-            quant("key", 1, dc)
+        for dc in range(2, 4):
+            for g in range(G):
+                ilv(key_raw, g, dc, "S")
+                quant("key", g, dc)
         for h in range(2):
             for g in range(G):
                 out_units(1, g, [(j, 2 * h + e) for j in range(J) for e in range(2)], "V")

@@ -51,8 +51,9 @@ def tile_memory_pa_v_kernel(tc, memory, key, strength, sharpen, sim, w, grad_out
         slot_scales = keep.tile([P, G, N], U8, name="slot_scales", align_bytes=64)
         squares = keep.tile([P, D], BF16, name="squares")
         minv_row = keep.tile([P, N], F32, name="minv_row")
+        ident_bf = keep.tile([P, P], BF16, name="ident_bf")
+        products = keep.tile([P, N], BF16, name="products")
         ident = keep.tile([P, P], F32, name="ident")
-        products = keep.tile([P, P], BF16, name="products")
         ones = keep.tile([P, 1], F32, name="ones")
         half = keep.tile([P, 8], F32, name="half")
         strength_sb = keep.tile([P, G, J], BF16, name="strength_sb")
@@ -69,18 +70,27 @@ def tile_memory_pa_v_kernel(tc, memory, key, strength, sharpen, sim, w, grad_out
         neg_rm = keep.tile([P, 8], F32, name="neg_rm")
         col_sum = keep.tile([P, 8], F32, name="col_sum")
 
-        w_sb, sim_sb, go_sb, wg_sb, dd_sb, grp = {}, {}, {}, {}, {}, {}
+        w_sb, sim_sb, go_sb, go_ps, dd_sb, grp, spread_ps, flip_ps, terms = {}, {}, {}, {}, {}, {}, {}, {}, {}
+
+        def grouped_tile(eng):
+            if eng == "V":
+                t = rows.tile([P, DC, J], BF16, name="grouped_v", bufs=2, align_bytes=64)
+            elif eng == "S":
+                t = rows.tile([P, DC, J], BF16, name="grouped_s", bufs=3, align_bytes=64)
+            else:
+                t = rows.tile([P, DC, J], BF16, name="grouped_g", bufs=1, align_bytes=64)
+            return t
 
         def load_w(g, j):
             w_sb[g, j] = rows.tile([P, N], F32, name="w_row")
             nc.sync.dma_start(out=w_sb[g, j][:], in_=w_hbm[:, g, j, :])
 
         def load_go(g, j):
-            go_sb[g, j] = rows.tile([P, N], BF16, name="go_row", bufs=4)
+            go_sb[g, j] = rows.tile([P, N], BF16, name="go_row", bufs=3)
             nc.sync.dma_start(out=go_sb[g, j][:], in_=go_hbm[:, g, j, :])
 
         def load_sim(g, j):
-            sim_sb[g, j] = rows.tile([P, N], F32, name="sim_row", bufs=5)
+            sim_sb[g, j] = rows.tile([P, N], F32, name="sim_row", bufs=4)
             nc.sync.dma_start(out=sim_sb[g, j][:], in_=sim_hbm[:, g, j, :])
 
         def load_mem(g, j):
@@ -93,50 +103,40 @@ def tile_memory_pa_v_kernel(tc, memory, key, strength, sharpen, sim, w, grad_out
             col = 4 * g + j
             nc.scalar.activation(out=squares[:], in_=raw[:, g, j, :], func=SQUARE, accum_out=ss[:, col : col + 1])
 
-        def gram(raw, ss, g, j):
-            words = raw[:, g, j, :].bitcast(F32)
-            turned = rows.tile([P, 8, P, 2], BF16, name="grouped", bufs=5, align_bytes=64)
-            turned_words = turned[:].rearrange("p k r e -> p (k r e)").bitcast(F32)
-            for h in range(2):
-                bank = psum.tile([P, 4, P], F32, name="flip", bufs=3)
-                for k in range(4):
-                    nc.tensor.transpose(bank[:, k, :], words[:, 128 * (4 * h + k) : 128 * (4 * h + k + 1)], ident[:])
-                nc.scalar.copy(out=turned_words[:, 512 * h : 512 * (h + 1)], in_=bank[:].rearrange("p k r -> p (k r)"))
-            acc = psum.tile([P, P], F32, name="acc")
-            for k in range(8):
-                for e in range(2):
-                    half_rows = turned[:, k, :, e]
-                    nc.tensor.matmul(acc[:], lhsT=half_rows, rhs=half_rows, start=(k == 0 and e == 0), stop=(k == 7 and e == 1))
-            col = 4 * g + j
-            nc.vector.scalar_tensor_tensor(
-                out=products[:], in0=acc[:], scalar=1.0, in1=ident[:], op0=MULT, op1=MULT, accum_out=ss[:, col : col + 1]
-            )
-
-        def inverse_norm(ss, inv, g):
+        def floor_ss(ss, g):
             cols = slice(4 * g, 4 * g + 4)
             nc.vector.tensor_scalar(out=ss[:, cols], in0=ss[:, cols], scalar1=1e-16, scalar2=None, op0=mybir.AluOpType.max)
+
+        def inverse_root(ss, inv, g):
+            cols = slice(4 * g, 4 * g + 4)
             nc.gpsimd.tensor_tensor(out=inv[:, cols], in0=ss[:, cols], in1=half[:, cols], op=mybir.AluOpType.pow)
 
-        def spread_minv(g):
-            bank = psum.tile([P, J, P], F32, name="flip", bufs=3)
+        def spread(g):
+            spread_ps[g] = psum.tile([P, J, P], F32, name="flip", bufs=3)
             for j in range(J):
                 col = 4 * g + j
-                nc.tensor.transpose(bank[:, j, :], mem_inv[:, col : col + 1].to_broadcast([P, P]), ident[:])
+                nc.tensor.transpose(spread_ps[g][:, j, :], mem_inv[:, col : col + 1].to_broadcast([P, P]), ident[:])
+
+        def keep_minv(g):
             nc.vector.tensor_copy(
-                out=minv_row[:, 512 * g : 512 * (g + 1)].rearrange("p (m j) -> p m j", j=J), in_=bank[:].rearrange("p j m -> p m j")
+                out=minv_row[:, 512 * g : 512 * (g + 1)].rearrange("p (m j) -> p m j", j=J), in_=spread_ps[g][:].rearrange("p j m -> p m j")
             )
+
+        def lift(g, j):
+            go_ps[g, j] = psum.tile([P, N], BF16, name="flip", bufs=3)
+            for h in range(2):
+                nc.tensor.matmul(go_ps[g, j][:, 512 * h : 512 * (h + 1)], lhsT=ident_bf[:], rhs=go_sb[g, j][:, 512 * h : 512 * (h + 1)], start=True, stop=True)
 
         def v1(g, j):
             col = 4 * g + j
-            wg_sb[g, j] = rows.tile([P, N], F32, name="wg_row", bufs=2)
             nc.vector.scalar_tensor_tensor(
-                out=wg_sb[g, j][:], in0=w_sb[g, j][:], scalar=-1.0, in1=go_sb[g, j][:], op0=MULT, op1=MULT, accum_out=neg_c[:, col : col + 1]
+                out=products[:], in0=w_sb[g, j][:], scalar=-1.0, in1=go_ps[g, j][:], op0=MULT, op1=MULT, accum_out=neg_c[:, col : col + 1]
             )
 
         def v2(g, j):
             col = 4 * g + j
             nc.vector.scalar_tensor_tensor(
-                out=w_sb[g, j][:], in0=w_sb[g, j][:], scalar=neg_c[:, col : col + 1], in1=wg_sb[g, j][:], op0=MULT, op1=SUB
+                out=w_sb[g, j][:], in0=go_ps[g, j][:], scalar=neg_c[:, col : col + 1], in1=w_sb[g, j][:], op0=ADD, op1=MULT
             )
 
         def v3(g, j):
@@ -160,23 +160,30 @@ def tile_memory_pa_v_kernel(tc, memory, key, strength, sharpen, sim, w, grad_out
         def rk_of_group(g):
             cols = slice(4 * g, 4 * g + 4)
             nc.vector.scalar_tensor_tensor(out=neg_rk[:, cols], in0=row_sum[:, cols], scalar=-1.0, in1=key_inv[:, cols], op0=MULT, op1=MULT)
+
+        def rk_again(g):
+            cols = slice(4 * g, 4 * g + 4)
             nc.vector.tensor_mul(neg_rk[:, cols], neg_rk[:, cols], key_inv[:, cols])
 
-        def rm_of_all():
+        def rm_sum():
             nc.vector.tensor_reduce(out=col_sum[:], in_=sums[:], axis=mybir.AxisListType.X, op=ADD)
+
+        def rm_of_all():
             nc.vector.scalar_tensor_tensor(out=neg_rm[:], in0=col_sum[:], scalar=-1.0, in1=mem_inv[:], op0=MULT, op1=MULT)
+
+        def rm_again():
             nc.vector.tensor_mul(neg_rm[:], neg_rm[:], mem_inv[:])
 
         def v4(g, j):
             col = 4 * g + j
-            if j == 0:
+            if g not in dd_sb:
                 dd_sb[g] = rows.tile([P, J, N], BF16, name="dd", bufs=1)
             nc.vector.scalar_tensor_tensor(
                 out=dd_sb[g][:, j, :], in0=w_sb[g, j][:], scalar=scl[:, col : col + 1], in1=minv_row[:], op0=MULT, op1=MULT
             )
 
         def ilv(raw, g, dc, eng):
-            t = rows.tile([P, DC, J], BF16, name="grouped", bufs=5, align_bytes=64)
+            t = grouped_tile(eng)
             grp["mem" if raw is mem_raw else "key", g, dc] = t
             out = t[:].rearrange("p (c i) j -> p c j i", i=4)
             in_ = raw[:, g, :, dc * DC : (dc + 1) * DC].rearrange("p j (c i) -> p c j i", i=4)
@@ -185,7 +192,10 @@ def tile_memory_pa_v_kernel(tc, memory, key, strength, sharpen, sim, w, grad_out
             elif eng == "V":
                 nc.vector.tensor_copy(out=out, in_=in_)
             else:
-                nc.gpsimd.tensor_scalar(out=out, in0=in_, scalar1=1.0, scalar2=0.0, op0=MULT, op1=ADD)
+                for s in range(4):
+                    nc.gpsimd.tensor_scalar(
+                        out=out[:, 32 * s : 32 * (s + 1)], in0=in_[:, 32 * s : 32 * (s + 1)], scalar1=1.0, scalar2=0.0, op0=MULT, op1=ADD
+                    )
 
         def quant(name, g, dc):
             codes, scales = (mem_codes, mem_scales) if name == "mem" else (key_codes, key_scales)
@@ -194,34 +204,40 @@ def tile_memory_pa_v_kernel(tc, memory, key, strength, sharpen, sim, w, grad_out
             nc.vector.quantize_mx(out=codes[:, g, cols].bitcast(E4M3), scales=scales[:, g, cols], in_=t[:].rearrange("p c j -> p (c j)"))
 
         def tok_ilv(g, q, eng):
-            t = rows.tile([P, DC, J], BF16, name="grouped", bufs=5, align_bytes=64)
+            t = grouped_tile(eng)
             grp["tok", g, q] = t
             out = t[:].rearrange("p (t m) j -> p t m j", t=J)
             in_ = dd_sb[g][:, :, 512 * q : 512 * (q + 1)].rearrange("p j (m t) -> p t m j", t=J)
             if eng == "V":
                 nc.vector.tensor_copy(out=out, in_=in_)
-            else:
+            elif eng == "S":
                 nc.scalar.copy(out=out, in_=in_)
+            else:
+                for t in range(J):
+                    nc.gpsimd.tensor_scalar(out=out[:, t], in0=in_[:, t], scalar1=1.0, scalar2=0.0, op0=MULT, op1=ADD)
 
         def tok_quant(g, q):
             cols = slice(512 * q, 512 * (q + 1))
             t = grp["tok", g, q]
             nc.vector.quantize_mx(out=tok_codes[:, g, cols].bitcast(E5M2), scales=tok_scales[:, g, cols], in_=t[:].rearrange("p c j -> p (c j)"))
 
-        def flip(g, q):
+        def flip(g, q, jj):
             words = dd_sb[g][:].rearrange("p j n -> p (j n)").bitcast(F32)
-            t = rows.tile([P, DC, J], BF16, name="grouped", bufs=5, align_bytes=64)
-            grp["slot", g, q] = t
-            t_words = t[:].rearrange("p c t -> p (c t)").bitcast(F32)
-            for jj in range(2):
-                bank = psum.tile([P, 2, 2, P], F32, name="flip", bufs=3)
-                for e in range(2):
-                    for v in range(2):
-                        first = 512 * (2 * jj + e) + 256 * q + v
-                        nc.tensor.transpose(bank[:, e, v, :], words[:, first : first + 255 : 2], ident[:])
-                nc.scalar.copy(
-                    out=t_words[:, 512 * jj : 512 * (jj + 1)].rearrange("p (e b v) -> p e b v", e=2, v=2), in_=bank[:].rearrange("p e v b -> p e b v")
-                )
+            bank = psum.tile([P, 2, 2, P], F32, name="flip", bufs=3)
+            flip_ps[g, q, jj] = bank
+            for e in range(2):
+                for v in range(2):
+                    first = 512 * (2 * jj + e) + 256 * q + v
+                    nc.tensor.transpose(bank[:, e, v, :], words[:, first : first + 255 : 2], ident[:])
+
+        def flip_copy(g, q, jj):
+            if ("slot", g, q) not in grp:
+                grp["slot", g, q] = grouped_tile("S")
+            t_words = grp["slot", g, q][:].rearrange("p c t -> p (c t)").bitcast(F32)
+            nc.scalar.copy(
+                out=t_words[:, 512 * jj : 512 * (jj + 1)].rearrange("p (e b v) -> p e b v", e=2, v=2),
+                in_=flip_ps[g, q, jj][:].rearrange("p e v b -> p e b v"),
+            )
 
         def slot_quant(g, q):
             cols = slice(512 * g, 512 * (g + 1))
@@ -246,147 +262,411 @@ def tile_memory_pa_v_kernel(tc, memory, key, strength, sharpen, sim, w, grad_out
 
         stage = {}
 
-        def v5(o, g, j, dc, eng="V"):
-            if dc % 2 == 0:
-                stage[o, g, j, dc // 2] = rows.tile([P, N], F32, name="w_row")
+        def half_stage(o, g, j, dc, eng):
+            if (o, g, j, dc // 2) not in stage:
+                if eng == "V":
+                    stage[o, g, j, dc // 2] = rows.tile([P, N], F32, name="w_row")
+                else:
+                    stage[o, g, j, dc // 2] = rows.tile([P, N], F32, name="stage_s", bufs=2)
+            h = dc % 2
+            return stage[o, g, j, dc // 2][:, h * DC : (h + 1) * DC]
+
+        def subtrahend(o, g, j, dc):
             col = 4 * g + j
             raw, neg = (key_raw, neg_rk) if o == 0 else (mem_raw, neg_rm)
-            h = dc % 2
-            out = stage[o, g, j, dc // 2][:, h * DC : (h + 1) * DC]
-            r = raw[:, g, j, dc * DC : (dc + 1) * DC]
-            n = neg[:, col : col + 1]
-            acc = accs[o, g, j, dc]
-            if eng == "V":
-                nc.vector.scalar_tensor_tensor(out=out, in0=r, scalar=n, in1=acc[:], op0=MULT, op1=ADD)
-            else:
-                nc.scalar.copy(out=out, in_=acc[:])
-                y = rows.tile([P, DC], F32, name="term", bufs=2)
-                if eng == "G":
-                    nc.gpsimd.tensor_scalar(out=y[:], in0=r, scalar1=n, scalar2=0.0, op0=MULT, op1=ADD)
-                else:
-                    nc.scalar.activation(out=y[:], in_=r, func=COPY, scale=n)
-                nc.gpsimd.tensor_tensor(out=out, in0=out, in1=y[:], op=ADD)
+            return raw[:, g, j, dc * DC : (dc + 1) * DC], neg[:, col : col + 1]
+
+        def v5(o, g, j, dc):
+            r, n = subtrahend(o, g, j, dc)
+            nc.vector.scalar_tensor_tensor(out=half_stage(o, g, j, dc, "V"), in0=r, scalar=n, in1=accs[o, g, j, dc][:], op0=MULT, op1=ADD)
+
+        def v5_take(o, g, j, dc):
+            nc.scalar.copy(out=half_stage(o, g, j, dc, "S"), in_=accs[o, g, j, dc][:])
+
+        def v5_term(o, g, j, dc):
+            r, n = subtrahend(o, g, j, dc)
+            terms[o, g, j, dc] = rows.tile([P, DC], F32, name="term", bufs=2)
+            nc.gpsimd.tensor_scalar(out=terms[o, g, j, dc][:], in0=r, scalar1=n, scalar2=0.0, op0=MULT, op1=ADD)
+
+        def v5_add(o, g, j, dc):
+            out = half_stage(o, g, j, dc, "S")
+            nc.gpsimd.tensor_tensor(out=out, in0=out, in1=terms[o, g, j, dc][:], op=ADD)
 
         def store(o, g, j, h):
             hbm = out_0_hbm if o == 0 else out_1_hbm
             nc.sync.dma_start(out=hbm[:, g, j, 2 * h * DC : 2 * (h + 1) * DC], in_=stage[o, g, j, h][:])
 
-        load_go(0, 0)
-        load_w(0, 0)
-        nc.sync.dma_start(out=strength_sb[:], in_=strength.rearrange("(g p j) o -> p g (j o)", p=P, j=J))
-        nc.sync.dma_start(out=sharpen_sb[:], in_=sharpen.rearrange("(g p j) o -> p g (j o)", p=P, j=J))
-        load_mem(0, 0)
-        load_mem(0, 1)
-        load_sim(0, 0)
-        load_mem(0, 2)
-        load_go(0, 1)
-        load_w(0, 1)
-        load_mem(0, 3)
-        load_sim(0, 1)
-        load_mem(1, 0)
-        load_go(0, 2)
-        load_w(0, 2)
-        load_mem(1, 1)
-        load_sim(0, 2)
+        sums = psum.tile([P, 8, 8], F32, name="sums", bufs=1)
+        ctx.enter_context(tc.manual_schedule())
         load_mem(1, 2)
-        load_go(0, 3)
-        load_w(0, 3)
+        nc.vector.memset(half[:], -0.5)
+        norm(mem_raw, mem_ss, 1, 2)
+        make_identity(nc, ident[:])
+        nc.vector.tensor_copy(out=ident_bf[:], in_=ident[:])
+        nc.vector.memset(ones[:], 1.0)
+        load_mem(1, 1)
         load_mem(1, 3)
-        load_sim(0, 3)
+        load_mem(1, 0)
+        ilv(mem_raw, 1, 0, "V")
+        load_go(0, 1)
+        load_go(1, 1)
+        lift(1, 1)
+        ilv(mem_raw, 1, 3, "V")
+        load_w(0, 1)
+        norm(mem_raw, mem_ss, 1, 1)
+        load_w(1, 1)
+        lift(0, 1)
+        v1(0, 1)
+        v1(1, 1)
+        v2(0, 1)
+        load_go(1, 3)
+        load_mem(0, 3)
+        ilv(mem_raw, 1, 1, "G")
+        nc.sync.dma_start(out=sharpen_sb[:], in_=sharpen.rearrange("(g p j) o -> p g (j o)", p=P, j=J))
+        nc.sync.dma_start(out=strength_sb[:], in_=strength.rearrange("(g p j) o -> p g (j o)", p=P, j=J))
+        quant("mem", 1, 3)
+        nc.vector.tensor_mul(fac[:], strength_sb[:].rearrange("p g j -> p (g j)"), sharpen_sb[:].rearrange("p g j -> p (g j)"))
+        load_w(0, 2)
+        norm(mem_raw, mem_ss, 1, 3)
+        norm(mem_raw, mem_ss, 1, 0)
+        floor_ss(mem_ss, 1)
+        load_mem(0, 2)
+        inverse_root(mem_ss, mem_inv, 1)
+        quant("mem", 1, 1)
+        quant("mem", 1, 0)
+        load_go(0, 2)
+        load_w(1, 3)
+        norm(mem_raw, mem_ss, 0, 3)
+        norm(mem_raw, mem_ss, 0, 2)
+        lift(0, 2)
+        load_mem(0, 1)
+        norm(mem_raw, mem_ss, 0, 1)
+        load_go(0, 0)
+        load_mem(0, 0)
+        v2(1, 1)
+        lift(1, 3)
         load_key(0, 0)
+        v1(0, 2)
+        ilv(mem_raw, 1, 2, "G")
+        v1(1, 3)
+        quant("mem", 1, 2)
+        norm(mem_raw, mem_ss, 0, 0)
+        v2(0, 2)
+        load_go(0, 3)
+        v2(1, 3)
+        load_w(0, 3)
+        norm(key_raw, key_ss, 0, 0)
+        lift(0, 3)
+        v1(0, 3)
+        ilv(mem_raw, 0, 2, "G")
+        quant("mem", 0, 2)
+        load_sim(0, 1)
+        v3(0, 1)
+        lift(0, 0)
+        load_sim(0, 2)
+        v3(0, 2)
+        colsum(0, 2)
+        load_w(0, 0)
+        floor_ss(mem_ss, 0)
+        spread(1)
+        ilv(mem_raw, 0, 0, "S")
+        v1(0, 0)
+        colsum(0, 1)
+        v2(0, 3)
+        v2(0, 0)
+        load_key(0, 2)
+        norm(key_raw, key_ss, 0, 2)
+        load_sim(0, 3)
+        v3(0, 3)
+        ilv(mem_raw, 0, 3, "G")
         load_key(0, 1)
+        norm(key_raw, key_ss, 0, 1)
+        keep_minv(1)
+        load_key(0, 3)
+        load_sim(0, 0)
+        v3(0, 0)
+        inverse_root(mem_ss, mem_inv, 0)
+        load_go(1, 2)
+        lift(1, 2)
+        load_w(1, 2)
+        v1(1, 2)
+        norm(key_raw, key_ss, 0, 3)
+        floor_ss(key_ss, 0)
+        load_key(1, 3)
+        spread(0)
+        keep_minv(0)
+        inverse_root(key_ss, key_inv, 0)
+        colsum(0, 0)
+        colsum(0, 3)
+        rk_of_group(0)
+        quant("mem", 0, 3)
+        rk_again(0)
+        v5_term(0, 0, 1, 1)
+        load_sim(1, 1)
+        v3(1, 1)
+        v5_term(0, 0, 1, 2)
+        scales_of_group(0)
+        quant("mem", 0, 0)
+        norm(key_raw, key_ss, 1, 3)
+        colsum(1, 1)
+        ilv(mem_raw, 0, 1, "S")
+        load_key(1, 0)
         load_go(1, 0)
         load_w(1, 0)
-        load_key(0, 2)
-        load_sim(1, 0)
-        load_key(0, 3)
-        load_go(1, 1)
-        load_w(1, 1)
-        load_key(1, 0)
-        load_sim(1, 1)
-        load_key(1, 1)
-        load_go(1, 2)
-        load_w(1, 2)
-        load_key(1, 2)
-        load_sim(1, 2)
-        load_key(1, 3)
-        load_go(1, 3)
-        load_w(1, 3)
+        norm(key_raw, key_ss, 1, 0)
+        v4(0, 3)
+        v4(0, 2)
+        flip(0, 0, 1)
+        flip_copy(0, 0, 1)
+        flip(0, 1, 1)
+        flip_copy(0, 1, 1)
+        v4(0, 0)
         load_sim(1, 3)
-        nc.vector.memset(half[:], -0.5)
-        nc.vector.memset(ones[:], 1.0)
-        make_identity(nc, ident[:])
-        sums = psum.tile([P, 8, 8], F32, name="sums", bufs=1)
-        nc.vector.tensor_mul(fac[:], strength_sb[:].rearrange("p g j -> p (g j)"), sharpen_sb[:].rearrange("p g j -> p (g j)"))
-
-        def elem(g, j):
-            v1(g, j)
-            v2(g, j)
-            v3(g, j)
-            colsum(g, j)
-
-        units = [(j, dc) for j in range(J) for dc in range(4)]
-
-        def out_units(o, g, items, engines):
-            for k, (j, dc) in enumerate(items):
-                mm(o, g, j, dc)
-                v5(o, g, j, dc, engines[k % len(engines)])
-                if dc % 2 == 1:
-                    store(o, g, j, dc // 2)
-
-        for j in range(J):
-            elem(0, j)
-            norm(mem_raw, mem_ss, 0, j)
-        inverse_norm(mem_ss, mem_inv, 0)
-        spread_minv(0)
-        for j in range(J):
-            norm(mem_raw, mem_ss, 1, j)
-        inverse_norm(mem_ss, mem_inv, 1)
-        spread_minv(1)
-        for j in range(J):
-            norm(key_raw, key_ss, 0, j)
-        inverse_norm(key_ss, key_inv, 0)
-        scales_of_group(0)
-        for j in range(J):
-            v4(0, j)
-        for q in range(G):
-            flip(0, q)
-            slot_quant(0, q)
-        rk_of_group(0)
-        for dc in range(4):
-            ilv(mem_raw, 0, dc, "VVVV"[dc])
-            quant("mem", 0, dc)
-            ilv(mem_raw, 1, dc, "SSSS"[dc])
-            quant("mem", 1, dc)
-        for j in range(J):
-            norm(key_raw, key_ss, 1, j)
-        inverse_norm(key_ss, key_inv, 1)
+        load_key(1, 2)
+        v4(0, 1)
+        flip(0, 1, 0)
+        v3(1, 3)
+        load_key(1, 1)
+        ilv(key_raw, 1, 2, "G")
+        quant("mem", 0, 1)
+        flip(0, 0, 0)
+        lift(1, 0)
+        flip_copy(0, 1, 0)
+        slot_quant(0, 1)
+        flip_copy(0, 0, 0)
+        slot_quant(0, 0)
+        mm(0, 0, 0, 0)
+        norm(key_raw, key_ss, 1, 1)
+        v2(1, 2)
+        mm(0, 0, 0, 1)
+        v1(1, 0)
+        v5(0, 0, 0, 1)
+        v2(1, 0)
+        mm(0, 0, 2, 0)
+        v5(0, 0, 2, 0)
+        norm(key_raw, key_ss, 1, 2)
+        floor_ss(key_ss, 1)
+        mm(0, 0, 1, 1)
+        load_sim(1, 2)
+        inverse_root(key_ss, key_inv, 1)
+        v3(1, 2)
+        v5(0, 0, 0, 0)
+        tok_ilv(0, 1, "S")
+        tok_quant(0, 1)
+        tok_ilv(0, 0, "S")
         scales_of_group(1)
-        for q in range(G):
-            tok_ilv(0, q, "S")
-            tok_quant(0, q)
-        for j in range(J):
-            elem(1, j)
-        for j in range(J):
-            v4(1, j)
-        for q in range(G):
-            flip(1, q)
-            slot_quant(1, q)
+        colsum(1, 3)
+        ilv(key_raw, 0, 2, "S")
+        mm(0, 0, 1, 0)
+        load_sim(1, 0)
+        v3(1, 0)
+        mm(0, 0, 1, 2)
+        v4(1, 3)
         rk_of_group(1)
-        out_units(0, 0, units, "V")
-        for q in range(G):
-            tok_ilv(1, q, "S")
-            tok_quant(1, q)
+        colsum(1, 2)
+        v5_take(0, 0, 1, 0)
+        mm(0, 0, 0, 2)
+        colsum(1, 0)
+        v4(1, 2)
+        v5(0, 0, 0, 2)
+        rm_sum()
+        v5_take(0, 0, 1, 1)
+        v4(1, 1)
+        mm(0, 0, 2, 1)
+        mm(0, 0, 0, 3)
+        v5(0, 0, 0, 3)
+        mm(0, 0, 3, 0)
+        v5(0, 0, 2, 1)
+        mm(0, 0, 1, 3)
+        v5_take(0, 0, 1, 2)
         rm_of_all()
-        for dc in range(2):
-            for g in range(G):
-                ilv(key_raw, g, dc, "S")
-                quant("key", g, dc)
-        out_units(0, 1, units, "V")
-        for dc in range(2, 4):
-            for g in range(G):
-                ilv(key_raw, g, dc, "S")
-                quant("key", g, dc)
-        for h in range(2):
-            for g in range(G):
-                out_units(1, g, [(j, 2 * h + e) for j in range(J) for e in range(2)], "V")
+        ilv(key_raw, 1, 3, "S")
+        mm(0, 0, 3, 1)
+        flip(1, 0, 1)
+        v5_add(0, 0, 1, 2)
+        rk_again(1)
+        v4(1, 0)
+        v5_term(0, 0, 1, 3)
+        v5_take(0, 0, 1, 3)
+        v5_add(0, 0, 1, 3)
+        rm_again()
+        tok_quant(0, 0)
+        flip_copy(1, 0, 1)
+        v5_term(0, 0, 1, 0)
+        mm(0, 0, 2, 3)
+        v5_add(0, 0, 1, 0)
+        flip(1, 1, 0)
+        quant("key", 1, 3)
+        flip(1, 1, 1)
+        flip_copy(1, 1, 0)
+        v5(0, 0, 3, 1)
+        v5_term(1, 0, 3, 3)
+        v5(0, 0, 3, 0)
+        v5(0, 0, 2, 3)
+        flip(1, 0, 0)
+        flip_copy(1, 0, 0)
+        slot_quant(1, 0)
+        flip_copy(1, 1, 1)
+        slot_quant(1, 1)
+        mm(0, 0, 3, 3)
+        v5(0, 0, 3, 3)
+        mm(0, 0, 2, 2)
+        v5(0, 0, 2, 2)
+        mm(0, 0, 3, 2)
+        v5(0, 0, 3, 2)
+        mm(0, 1, 2, 3)
+        v5(0, 1, 2, 3)
+        v5_add(0, 0, 1, 1)
+        mm(0, 1, 0, 1)
+        v5(0, 1, 0, 1)
+        mm(0, 1, 3, 3)
+        mm(0, 1, 0, 2)
+        v5(0, 1, 3, 3)
+        mm(0, 1, 0, 0)
+        ilv(key_raw, 0, 3, "S")
+        quant("key", 0, 3)
+        quant("key", 1, 2)
+        mm(0, 1, 0, 3)
+        tok_ilv(1, 0, "S")
+        tok_quant(1, 0)
+        mm(0, 1, 2, 2)
+        v5(0, 1, 2, 2)
+        v5(0, 1, 0, 0)
+        mm(0, 1, 1, 2)
+        v5(0, 1, 1, 2)
+        mm(0, 1, 1, 3)
+        quant("key", 0, 2)
+        mm(1, 0, 3, 3)
+        v5(0, 1, 1, 3)
+        v5_term(0, 1, 0, 3)
+        mm(0, 1, 2, 0)
+        v5(0, 1, 2, 0)
+        mm(1, 0, 2, 2)
+        v5(1, 0, 2, 2)
+        mm(1, 0, 3, 2)
+        mm(1, 0, 2, 3)
+        mm(1, 0, 0, 3)
+        mm(1, 0, 0, 2)
+        v5_take(0, 1, 0, 3)
+        tok_ilv(1, 1, "S")
+        tok_quant(1, 1)
+        v5(1, 0, 2, 3)
+        v5(1, 0, 0, 3)
+        mm(0, 1, 2, 1)
+        v5(0, 1, 2, 1)
+        v5_add(0, 1, 0, 3)
+        mm(0, 1, 3, 1)
+        v5(1, 0, 0, 2)
+        mm(0, 1, 3, 2)
+        v5_take(0, 1, 0, 2)
+        v5(0, 1, 3, 1)
+        v5(0, 1, 3, 2)
+        v5_term(0, 1, 0, 2)
+        v5_add(0, 1, 0, 2)
+        v5_take(1, 0, 3, 3)
+        mm(1, 1, 2, 3)
+        v5(1, 1, 2, 3)
+        mm(1, 1, 2, 2)
+        mm(1, 0, 1, 3)
+        v5(1, 1, 2, 2)
+        mm(1, 1, 0, 3)
+        mm(1, 0, 1, 2)
+        v5(1, 0, 1, 3)
+        mm(0, 1, 3, 0)
+        mm(0, 1, 1, 0)
+        v5(1, 0, 1, 2)
+        mm(1, 1, 3, 3)
+        mm(1, 1, 3, 2)
+        mm(0, 1, 1, 1)
+        v5(0, 1, 3, 0)
+        mm(1, 1, 0, 2)
+        v5_take(1, 0, 3, 2)
+        mm(1, 1, 1, 2)
+        v5_term(1, 0, 3, 2)
+        v5_add(1, 0, 3, 2)
+        v5(0, 1, 1, 0)
+        v5(1, 1, 0, 3)
+        ilv(key_raw, 0, 1, "S")
+        quant("key", 0, 1)
+        mm(1, 1, 1, 3)
+        ilv(key_raw, 1, 1, "S")
+        quant("key", 1, 1)
+        v5_add(1, 0, 3, 3)
+        v5(0, 1, 1, 1)
+        mm(1, 1, 3, 1)
+        v5(1, 1, 0, 2)
+        v5(1, 1, 1, 2)
+        v5(1, 1, 1, 3)
+        ilv(key_raw, 1, 0, "G")
+        quant("key", 1, 0)
+        mm(1, 1, 0, 1)
+        store(0, 0, 0, 0)
+        ilv(key_raw, 0, 0, "S")
+        quant("key", 0, 0)
+        v5(1, 1, 0, 1)
+        mm(1, 1, 3, 0)
+        mm(1, 1, 0, 0)
+        mm(1, 1, 2, 1)
+        v5(1, 1, 3, 1)
+        v5(1, 1, 3, 0)
+        v5(1, 1, 0, 0)
+        mm(1, 1, 2, 0)
+        v5(1, 1, 2, 1)
+        v5(1, 1, 2, 0)
+        v5_take(1, 1, 3, 3)
+        mm(1, 1, 1, 0)
+        v5_term(1, 1, 3, 2)
+        mm(1, 0, 2, 0)
+        v5_term(1, 1, 3, 3)
+        store(0, 0, 0, 1)
+        v5(1, 0, 2, 0)
+        mm(1, 0, 2, 1)
+        v5(1, 0, 2, 1)
+        store(0, 0, 2, 0)
+        v5(1, 1, 1, 0)
+        mm(1, 1, 1, 1)
+        store(0, 0, 3, 0)
+        mm(1, 0, 3, 1)
+        v5_take(1, 1, 3, 2)
+        v5(1, 1, 1, 1)
+        mm(1, 0, 3, 0)
+        v5_add(1, 1, 3, 2)
+        mm(1, 0, 0, 1)
+        store(0, 0, 1, 1)
+        store(0, 0, 2, 1)
+        v5(1, 0, 3, 0)
+        mm(1, 0, 1, 0)
+        v5(1, 0, 3, 1)
+        v5_add(1, 1, 3, 3)
+        store(0, 0, 3, 1)
+        store(0, 0, 1, 0)
+        store(0, 1, 2, 1)
+        store(0, 1, 0, 0)
+        store(0, 1, 1, 1)
+        mm(1, 0, 0, 0)
+        store(0, 1, 0, 1)
+        v5(1, 0, 0, 1)
+        store(1, 0, 2, 1)
+        store(0, 1, 2, 0)
+        v5(1, 0, 0, 0)
+        store(1, 0, 3, 1)
+        store(1, 0, 0, 1)
+        store(1, 1, 2, 1)
+        store(0, 1, 3, 1)
+        store(1, 0, 1, 1)
+        store(0, 1, 3, 0)
+        store(0, 1, 1, 0)
+        store(1, 1, 0, 1)
+        store(1, 1, 1, 1)
+        mm(1, 0, 1, 1)
+        store(1, 1, 3, 1)
+        store(1, 1, 3, 0)
+        store(1, 1, 0, 0)
+        v5(1, 0, 1, 0)
+        store(1, 1, 2, 0)
+        store(1, 0, 2, 0)
+        v5(1, 0, 1, 1)
+        store(1, 1, 1, 0)
+        store(1, 0, 3, 0)
+        store(1, 0, 0, 0)
+        store(1, 0, 1, 0)

@@ -37,7 +37,7 @@ def tile_memory_pa_v_kernel(tc, memory, key, strength, sharpen, sim, w, grad_out
     with ExitStack() as ctx:
         keep = ctx.enter_context(tc.tile_pool(name="keep", bufs=1))
         rows = ctx.enter_context(tc.tile_pool(name="rows", bufs=8))
-        psum = ctx.enter_context(tc.psum_pool(name="psum", bufs=4))
+        psum = ctx.enter_context(tc.psum_pool(name="psum", bufs=5))
 
         mem_raw = keep.tile([P, G, J, D], BF16, name="mem_raw")
         key_raw = keep.tile([P, G, J, D], BF16, name="key_raw")
@@ -51,8 +51,6 @@ def tile_memory_pa_v_kernel(tc, memory, key, strength, sharpen, sim, w, grad_out
         slot_scales = keep.tile([P, G, N], U8, name="slot_scales", align_bytes=64)
         squares = keep.tile([P, D], BF16, name="squares")
         minv_row = keep.tile([P, N], F32, name="minv_row")
-        ident_bf = keep.tile([P, P], BF16, name="ident_bf")
-        products = keep.tile([P, N], BF16, name="products")
         ident = keep.tile([P, P], F32, name="ident")
         ones = keep.tile([P, 1], F32, name="ones")
         half = keep.tile([P, 8], F32, name="half")
@@ -70,34 +68,35 @@ def tile_memory_pa_v_kernel(tc, memory, key, strength, sharpen, sim, w, grad_out
         neg_rm = keep.tile([P, 8], F32, name="neg_rm")
         col_sum = keep.tile([P, 8], F32, name="col_sum")
 
-        w_sb, sim_sb, go_sb, go_ps, dd_sb, grp, spread_ps, flip_ps, terms = {}, {}, {}, {}, {}, {}, {}, {}, {}
+        w_sb, sim_sb, go_sb, wg_sb, dd_sb, grp, go_pairs, spread_ps, flip_ps, terms = {}, {}, {}, {}, {}, {}, {}, {}, {}, {}
 
         def grouped_tile(eng):
             if eng == "V":
                 t = rows.tile([P, DC, J], BF16, name="grouped_v", bufs=2, align_bytes=64)
-            elif eng == "S":
-                t = rows.tile([P, DC, J], BF16, name="grouped_s", bufs=3, align_bytes=64)
             else:
-                t = rows.tile([P, DC, J], BF16, name="grouped_g", bufs=1, align_bytes=64)
+                t = rows.tile([P, DC, J], BF16, name="grouped_s", bufs=3, align_bytes=64)
             return t
 
         def load_w(g, j):
             w_sb[g, j] = rows.tile([P, N], F32, name="w_row")
             nc.sync.dma_start(out=w_sb[g, j][:], in_=w_hbm[:, g, j, :])
 
-        def load_go(g, j):
-            go_sb[g, j] = rows.tile([P, N], BF16, name="go_row", bufs=3)
-            nc.sync.dma_start(out=go_sb[g, j][:], in_=go_hbm[:, g, j, :])
+        def load_go(g, j, count):
+            if (g, j // 2) not in go_pairs:
+                go_pairs[g, j // 2] = rows.tile([P, 2, N], BF16, name="go_pair", bufs=2)
+            for i in range(j, j + count):
+                go_sb[g, i] = go_pairs[g, j // 2][:, i % 2, :]
+            nc.sync.dma_start(out=go_pairs[g, j // 2][:, j % 2 : j % 2 + count, :], in_=go_hbm[:, g, j : j + count, :])
 
         def load_sim(g, j):
             sim_sb[g, j] = rows.tile([P, N], F32, name="sim_row", bufs=4)
             nc.sync.dma_start(out=sim_sb[g, j][:], in_=sim_hbm[:, g, j, :])
 
-        def load_mem(g, j):
-            nc.sync.dma_start(out=mem_raw[:, g, j, :], in_=mem_hbm[:, g, j, :])
+        def load_mem(g, j, count):
+            nc.sync.dma_start(out=mem_raw[:, g, j : j + count, :], in_=mem_hbm[:, g, j : j + count, :])
 
-        def load_key(g, j):
-            nc.sync.dma_start(out=key_raw[:, g, j, :], in_=key_hbm[:, g, j, :])
+        def load_key(g, j, count):
+            nc.sync.dma_start(out=key_raw[:, g, j : j + count, :], in_=key_hbm[:, g, j : j + count, :])
 
         def norm(raw, ss, g, j):
             col = 4 * g + j
@@ -112,7 +111,7 @@ def tile_memory_pa_v_kernel(tc, memory, key, strength, sharpen, sim, w, grad_out
             nc.gpsimd.tensor_tensor(out=inv[:, cols], in0=ss[:, cols], in1=half[:, cols], op=mybir.AluOpType.pow)
 
         def spread(g):
-            spread_ps[g] = psum.tile([P, J, P], F32, name="flip", bufs=3)
+            spread_ps[g] = psum.tile([P, J, P], F32, name="flip", bufs=2)
             for j in range(J):
                 col = 4 * g + j
                 nc.tensor.transpose(spread_ps[g][:, j, :], mem_inv[:, col : col + 1].to_broadcast([P, P]), ident[:])
@@ -122,21 +121,17 @@ def tile_memory_pa_v_kernel(tc, memory, key, strength, sharpen, sim, w, grad_out
                 out=minv_row[:, 512 * g : 512 * (g + 1)].rearrange("p (m j) -> p m j", j=J), in_=spread_ps[g][:].rearrange("p j m -> p m j")
             )
 
-        def lift(g, j):
-            go_ps[g, j] = psum.tile([P, N], BF16, name="flip", bufs=3)
-            for h in range(2):
-                nc.tensor.matmul(go_ps[g, j][:, 512 * h : 512 * (h + 1)], lhsT=ident_bf[:], rhs=go_sb[g, j][:, 512 * h : 512 * (h + 1)], start=True, stop=True)
-
         def v1(g, j):
             col = 4 * g + j
+            wg_sb[g, j] = rows.tile([P, N], F32, name="wg_row", bufs=2)
             nc.vector.scalar_tensor_tensor(
-                out=products[:], in0=w_sb[g, j][:], scalar=-1.0, in1=go_ps[g, j][:], op0=MULT, op1=MULT, accum_out=neg_c[:, col : col + 1]
+                out=wg_sb[g, j][:], in0=w_sb[g, j][:], scalar=-1.0, in1=go_sb[g, j][:], op0=MULT, op1=MULT, accum_out=neg_c[:, col : col + 1]
             )
 
         def v2(g, j):
             col = 4 * g + j
             nc.vector.scalar_tensor_tensor(
-                out=w_sb[g, j][:], in0=go_ps[g, j][:], scalar=neg_c[:, col : col + 1], in1=w_sb[g, j][:], op0=ADD, op1=MULT
+                out=w_sb[g, j][:], in0=w_sb[g, j][:], scalar=neg_c[:, col : col + 1], in1=wg_sb[g, j][:], op0=MULT, op1=SUB
             )
 
         def v3(g, j):
@@ -210,11 +205,8 @@ def tile_memory_pa_v_kernel(tc, memory, key, strength, sharpen, sim, w, grad_out
             in_ = dd_sb[g][:, :, 512 * q : 512 * (q + 1)].rearrange("p j (m t) -> p t m j", t=J)
             if eng == "V":
                 nc.vector.tensor_copy(out=out, in_=in_)
-            elif eng == "S":
-                nc.scalar.copy(out=out, in_=in_)
             else:
-                for t in range(J):
-                    nc.gpsimd.tensor_scalar(out=out[:, t], in0=in_[:, t], scalar1=1.0, scalar2=0.0, op0=MULT, op1=ADD)
+                nc.scalar.copy(out=out, in_=in_)
 
         def tok_quant(g, q):
             cols = slice(512 * q, 512 * (q + 1))
@@ -223,7 +215,7 @@ def tile_memory_pa_v_kernel(tc, memory, key, strength, sharpen, sim, w, grad_out
 
         def flip(g, q, jj):
             words = dd_sb[g][:].rearrange("p j n -> p (j n)").bitcast(F32)
-            bank = psum.tile([P, 2, 2, P], F32, name="flip", bufs=3)
+            bank = psum.tile([P, 2, 2, P], F32, name="flip", bufs=2)
             flip_ps[g, q, jj] = bank
             for e in range(2):
                 for v in range(2):
@@ -298,375 +290,360 @@ def tile_memory_pa_v_kernel(tc, memory, key, strength, sharpen, sim, w, grad_out
 
         sums = psum.tile([P, 8, 8], F32, name="sums", bufs=1)
         ctx.enter_context(tc.manual_schedule())
-        load_mem(1, 2)
-        nc.vector.memset(half[:], -0.5)
-        norm(mem_raw, mem_ss, 1, 2)
-        make_identity(nc, ident[:])
-        nc.vector.tensor_copy(out=ident_bf[:], in_=ident[:])
-        nc.vector.memset(ones[:], 1.0)
-        load_mem(1, 1)
-        load_mem(1, 3)
-        load_mem(1, 0)
-        ilv(mem_raw, 1, 0, "V")
-        load_go(0, 1)
-        load_go(1, 1)
-        lift(1, 1)
-        ilv(mem_raw, 1, 3, "V")
-        load_w(0, 1)
+        load_mem(1, 0, 2)
         norm(mem_raw, mem_ss, 1, 1)
-        load_w(1, 1)
-        lift(0, 1)
-        v1(0, 1)
-        v1(1, 1)
-        v2(0, 1)
-        load_go(1, 3)
-        load_mem(0, 3)
-        ilv(mem_raw, 1, 1, "G")
-        nc.sync.dma_start(out=sharpen_sb[:], in_=sharpen.rearrange("(g p j) o -> p g (j o)", p=P, j=J))
-        nc.sync.dma_start(out=strength_sb[:], in_=strength.rearrange("(g p j) o -> p g (j o)", p=P, j=J))
-        quant("mem", 1, 3)
-        nc.vector.tensor_mul(fac[:], strength_sb[:].rearrange("p g j -> p (g j)"), sharpen_sb[:].rearrange("p g j -> p (g j)"))
-        load_w(0, 2)
-        norm(mem_raw, mem_ss, 1, 3)
-        norm(mem_raw, mem_ss, 1, 0)
-        floor_ss(mem_ss, 1)
-        load_mem(0, 2)
-        inverse_root(mem_ss, mem_inv, 1)
-        quant("mem", 1, 1)
-        quant("mem", 1, 0)
-        load_go(0, 2)
-        load_w(1, 3)
-        norm(mem_raw, mem_ss, 0, 3)
-        norm(mem_raw, mem_ss, 0, 2)
-        lift(0, 2)
-        load_mem(0, 1)
-        norm(mem_raw, mem_ss, 0, 1)
-        load_go(0, 0)
-        load_mem(0, 0)
-        v2(1, 1)
-        lift(1, 3)
-        load_key(0, 0)
-        v1(0, 2)
-        ilv(mem_raw, 1, 2, "G")
-        v1(1, 3)
+        nc.vector.memset(half[:], -0.5)
+        load_mem(1, 2, 2)
+        ilv(mem_raw, 1, 1, "V")
+        ilv(mem_raw, 1, 3, "V")
+        ilv(mem_raw, 1, 2, "S")
         quant("mem", 1, 2)
-        norm(mem_raw, mem_ss, 0, 0)
-        v2(0, 2)
-        load_go(0, 3)
-        v2(1, 3)
+        quant("mem", 1, 3)
+        load_mem(0, 2, 2)
+        norm(mem_raw, mem_ss, 0, 3)
+        load_mem(0, 1, 1)
+        quant("mem", 1, 1)
+        norm(mem_raw, mem_ss, 1, 0)
+        load_mem(0, 0, 1)
+        norm(mem_raw, mem_ss, 1, 3)
+        ilv(mem_raw, 0, 3, "V")
+        nc.sync.dma_start(out=sharpen_sb[:], in_=sharpen.rearrange("(g p j) o -> p g (j o)", p=P, j=J))
+        make_identity(nc, ident[:])
+        nc.sync.dma_start(out=strength_sb[:], in_=strength.rearrange("(g p j) o -> p g (j o)", p=P, j=J))
+        load_go(0, 2, 2)
+        load_w(0, 2)
         load_w(0, 3)
-        norm(key_raw, key_ss, 0, 0)
-        lift(0, 3)
+        nc.vector.tensor_mul(fac[:], strength_sb[:].rearrange("p g j -> p (g j)"), sharpen_sb[:].rearrange("p g j -> p (g j)"))
+        load_sim(0, 3)
+        ilv(mem_raw, 0, 1, "V")
+        v1(0, 2)
         v1(0, 3)
-        ilv(mem_raw, 0, 2, "G")
-        quant("mem", 0, 2)
+        v2(0, 2)
+        v2(0, 3)
+        load_sim(0, 2)
+        load_w(0, 1)
+        load_go(0, 1, 1)
+        v1(0, 1)
+        quant("mem", 0, 3)
+        nc.vector.memset(ones[:], 1.0)
+        norm(mem_raw, mem_ss, 0, 0)
+        v3(0, 3)
+        v2(0, 1)
+        norm(mem_raw, mem_ss, 1, 2)
+        v3(0, 2)
+        load_w(1, 0)
         load_sim(0, 1)
         v3(0, 1)
-        lift(0, 0)
-        load_sim(0, 2)
-        v3(0, 2)
-        colsum(0, 2)
+        load_go(0, 0, 1)
         load_w(0, 0)
-        floor_ss(mem_ss, 0)
-        spread(1)
-        ilv(mem_raw, 0, 0, "S")
         v1(0, 0)
-        colsum(0, 1)
-        v2(0, 3)
-        v2(0, 0)
-        load_key(0, 2)
+        load_key(0, 2, 2)
+        colsum(0, 3)
+        colsum(0, 2)
+        norm(mem_raw, mem_ss, 0, 2)
+        norm(mem_raw, mem_ss, 0, 1)
+        floor_ss(mem_ss, 0)
+        inverse_root(mem_ss, mem_inv, 0)
+        floor_ss(mem_ss, 1)
+        spread(0)
         norm(key_raw, key_ss, 0, 2)
-        load_sim(0, 3)
-        v3(0, 3)
-        ilv(mem_raw, 0, 3, "G")
-        load_key(0, 1)
-        norm(key_raw, key_ss, 0, 1)
-        keep_minv(1)
-        load_key(0, 3)
+        inverse_root(mem_ss, mem_inv, 1)
+        spread(1)
+        quant("mem", 0, 1)
+        norm(key_raw, key_ss, 0, 3)
+        v2(0, 0)
         load_sim(0, 0)
         v3(0, 0)
-        inverse_root(mem_ss, mem_inv, 0)
-        load_go(1, 2)
-        lift(1, 2)
-        load_w(1, 2)
-        v1(1, 2)
-        norm(key_raw, key_ss, 0, 3)
-        floor_ss(key_ss, 0)
-        load_key(1, 3)
-        spread(0)
-        keep_minv(0)
-        inverse_root(key_ss, key_inv, 0)
+        load_go(1, 0, 2)
         colsum(0, 0)
-        colsum(0, 3)
-        rk_of_group(0)
-        quant("mem", 0, 3)
-        rk_again(0)
-        v5_term(0, 0, 1, 1)
-        load_sim(1, 1)
-        v3(1, 1)
-        v5_term(0, 0, 1, 2)
+        v1(1, 0)
+        load_key(0, 0, 2)
+        norm(key_raw, key_ss, 0, 0)
+        keep_minv(0)
+        load_w(1, 1)
+        load_w(1, 2)
+        v1(1, 1)
+        v2(1, 0)
+        norm(key_raw, key_ss, 0, 1)
+        floor_ss(key_ss, 0)
+        keep_minv(1)
+        inverse_root(key_ss, key_inv, 0)
+        load_sim(1, 0)
         scales_of_group(0)
-        quant("mem", 0, 0)
-        norm(key_raw, key_ss, 1, 3)
-        colsum(1, 1)
-        ilv(mem_raw, 0, 1, "S")
-        load_key(1, 0)
-        load_go(1, 0)
-        load_w(1, 0)
-        norm(key_raw, key_ss, 1, 0)
+        colsum(0, 1)
+        rk_of_group(0)
+        rk_again(0)
         v4(0, 3)
+        load_key(1, 2, 2)
+        load_go(1, 2, 2)
         v4(0, 2)
         flip(0, 0, 1)
+        v4(0, 1)
+        v4(0, 0)
+        ilv(mem_raw, 0, 2, "S")
+        norm(key_raw, key_ss, 1, 2)
+        v2(1, 1)
+        quant("mem", 0, 2)
+        v5_term(0, 0, 1, 2)
+        load_key(1, 0, 2)
         flip_copy(0, 0, 1)
         flip(0, 1, 1)
         flip_copy(0, 1, 1)
-        v4(0, 0)
-        load_sim(1, 3)
-        load_key(1, 2)
-        v4(0, 1)
+        load_sim(1, 1)
+        norm(key_raw, key_ss, 1, 0)
+        v3(1, 1)
         flip(0, 1, 0)
-        v3(1, 3)
-        load_key(1, 1)
-        ilv(key_raw, 1, 2, "G")
-        quant("mem", 0, 1)
-        flip(0, 0, 0)
-        lift(1, 0)
         flip_copy(0, 1, 0)
+        flip(0, 0, 0)
+        load_w(1, 3)
+        v1(1, 3)
         slot_quant(0, 1)
         flip_copy(0, 0, 0)
+        colsum(1, 1)
         slot_quant(0, 0)
-        mm(0, 0, 0, 0)
-        norm(key_raw, key_ss, 1, 1)
+        mm(0, 0, 0, 3)
+        v1(1, 2)
+        v5_term(0, 0, 1, 3)
+        mm(0, 0, 0, 2)
+        mm(0, 0, 1, 2)
+        mm(0, 0, 2, 3)
+        mm(0, 0, 3, 1)
+        ilv(mem_raw, 1, 0, "S")
+        v5(0, 0, 0, 3)
+        v5(0, 0, 0, 2)
+        ilv(mem_raw, 0, 0, "S")
         v2(1, 2)
-        mm(0, 0, 0, 1)
-        v1(1, 0)
-        v5(0, 0, 0, 1)
-        v2(1, 0)
-        mm(0, 0, 2, 0)
-        v5(0, 0, 2, 0)
-        norm(key_raw, key_ss, 1, 2)
-        floor_ss(key_ss, 1)
-        mm(0, 0, 1, 1)
+        quant("mem", 0, 0)
         load_sim(1, 2)
-        inverse_root(key_ss, key_inv, 1)
+        norm(key_raw, key_ss, 1, 3)
+        quant("mem", 1, 0)
         v3(1, 2)
-        v5(0, 0, 0, 0)
+        colsum(1, 2)
+        mm(0, 0, 1, 1)
+        v2(1, 3)
+        mm(0, 0, 2, 0)
+        v3(1, 0)
+        v5(0, 0, 2, 3)
+        norm(key_raw, key_ss, 1, 1)
+        floor_ss(key_ss, 1)
+        load_sim(1, 3)
+        v3(1, 3)
+        mm(0, 0, 3, 0)
+        v5(0, 0, 3, 0)
+        inverse_root(key_ss, key_inv, 1)
+        scales_of_group(1)
+        tok_ilv(0, 0, "S")
+        tok_quant(0, 0)
+        colsum(1, 3)
+        rk_of_group(1)
+        v5(0, 0, 2, 0)
+        v4(1, 1)
+        v4(1, 0)
         tok_ilv(0, 1, "S")
         tok_quant(0, 1)
-        tok_ilv(0, 0, "S")
-        scales_of_group(1)
-        colsum(1, 3)
-        ilv(key_raw, 0, 2, "S")
-        mm(0, 0, 1, 0)
-        load_sim(1, 0)
-        v3(1, 0)
-        mm(0, 0, 1, 2)
-        v4(1, 3)
-        rk_of_group(1)
-        colsum(1, 2)
-        v5_take(0, 0, 1, 0)
-        mm(0, 0, 0, 2)
-        colsum(1, 0)
+        ilv(key_raw, 1, 0, "S")
         v4(1, 2)
-        v5(0, 0, 0, 2)
+        colsum(1, 0)
+        quant("key", 1, 0)
         rm_sum()
-        v5_take(0, 0, 1, 1)
-        v4(1, 1)
-        mm(0, 0, 2, 1)
-        mm(0, 0, 0, 3)
-        v5(0, 0, 0, 3)
-        mm(0, 0, 3, 0)
-        v5(0, 0, 2, 1)
-        mm(0, 0, 1, 3)
-        v5_take(0, 0, 1, 2)
-        rm_of_all()
-        ilv(key_raw, 1, 3, "S")
-        mm(0, 0, 3, 1)
-        flip(1, 0, 1)
-        v5_add(0, 0, 1, 2)
-        rk_again(1)
-        v4(1, 0)
-        v5_term(0, 0, 1, 3)
-        v5_take(0, 0, 1, 3)
-        v5_add(0, 0, 1, 3)
-        rm_again()
-        tok_quant(0, 0)
-        flip_copy(1, 0, 1)
-        v5_term(0, 0, 1, 0)
-        mm(0, 0, 2, 3)
-        v5_add(0, 0, 1, 0)
-        flip(1, 1, 0)
-        quant("key", 1, 3)
-        flip(1, 1, 1)
-        flip_copy(1, 1, 0)
-        v5(0, 0, 3, 1)
-        v5_term(1, 0, 3, 3)
-        v5(0, 0, 3, 0)
-        v5(0, 0, 2, 3)
         flip(1, 0, 0)
-        flip_copy(1, 0, 0)
-        slot_quant(1, 0)
-        flip_copy(1, 1, 1)
-        slot_quant(1, 1)
-        mm(0, 0, 3, 3)
-        v5(0, 0, 3, 3)
-        mm(0, 0, 2, 2)
-        v5(0, 0, 2, 2)
-        mm(0, 0, 3, 2)
-        v5(0, 0, 3, 2)
-        mm(0, 1, 2, 3)
-        v5(0, 1, 2, 3)
-        v5_add(0, 0, 1, 1)
-        mm(0, 1, 0, 1)
-        v5(0, 1, 0, 1)
-        mm(0, 1, 3, 3)
-        mm(0, 1, 0, 2)
-        v5(0, 1, 3, 3)
-        mm(0, 1, 0, 0)
-        ilv(key_raw, 0, 3, "S")
-        quant("key", 0, 3)
-        quant("key", 1, 2)
-        mm(0, 1, 0, 3)
-        tok_ilv(1, 0, "S")
-        tok_quant(1, 0)
-        mm(0, 1, 2, 2)
-        v5(0, 1, 2, 2)
-        v5(0, 1, 0, 0)
-        mm(0, 1, 1, 2)
-        v5(0, 1, 1, 2)
-        mm(0, 1, 1, 3)
-        quant("key", 0, 2)
-        mm(1, 0, 3, 3)
-        v5(0, 1, 1, 3)
-        v5_term(0, 1, 0, 3)
-        mm(0, 1, 2, 0)
-        v5(0, 1, 2, 0)
-        mm(1, 0, 2, 2)
-        v5(1, 0, 2, 2)
-        mm(1, 0, 3, 2)
-        mm(1, 0, 2, 3)
-        mm(1, 0, 0, 3)
-        mm(1, 0, 0, 2)
-        v5_take(0, 1, 0, 3)
-        tok_ilv(1, 1, "S")
-        tok_quant(1, 1)
-        v5(1, 0, 2, 3)
-        v5(1, 0, 0, 3)
-        mm(0, 1, 2, 1)
-        v5(0, 1, 2, 1)
-        v5_add(0, 1, 0, 3)
-        mm(0, 1, 3, 1)
-        v5(1, 0, 0, 2)
-        mm(0, 1, 3, 2)
-        v5_take(0, 1, 0, 2)
-        v5(0, 1, 3, 1)
-        v5(0, 1, 3, 2)
-        v5_term(0, 1, 0, 2)
-        v5_add(0, 1, 0, 2)
-        v5_take(1, 0, 3, 3)
-        mm(1, 1, 2, 3)
-        v5(1, 1, 2, 3)
-        mm(1, 1, 2, 2)
-        mm(1, 0, 1, 3)
-        v5(1, 1, 2, 2)
-        mm(1, 1, 0, 3)
-        mm(1, 0, 1, 2)
-        v5(1, 0, 1, 3)
-        mm(0, 1, 3, 0)
-        mm(0, 1, 1, 0)
-        v5(1, 0, 1, 2)
-        mm(1, 1, 3, 3)
-        mm(1, 1, 3, 2)
-        mm(0, 1, 1, 1)
-        v5(0, 1, 3, 0)
-        mm(1, 1, 0, 2)
-        v5_take(1, 0, 3, 2)
-        mm(1, 1, 1, 2)
-        v5_term(1, 0, 3, 2)
-        v5_add(1, 0, 3, 2)
-        v5(0, 1, 1, 0)
-        v5(1, 1, 0, 3)
-        ilv(key_raw, 0, 1, "S")
-        quant("key", 0, 1)
-        mm(1, 1, 1, 3)
+        v4(1, 3)
         ilv(key_raw, 1, 1, "S")
         quant("key", 1, 1)
-        v5_add(1, 0, 3, 3)
-        v5(0, 1, 1, 1)
-        mm(1, 1, 3, 1)
-        v5(1, 1, 0, 2)
-        v5(1, 1, 1, 2)
-        v5(1, 1, 1, 3)
-        ilv(key_raw, 1, 0, "G")
-        quant("key", 1, 0)
-        mm(1, 1, 0, 1)
-        store(0, 0, 0, 0)
+        flip(1, 1, 0)
+        flip_copy(1, 0, 0)
+        v5_take(0, 0, 1, 2)
+        flip_copy(1, 1, 0)
+        mm(0, 0, 0, 0)
+        rm_of_all()
+        mm(0, 0, 1, 3)
+        v5(0, 0, 0, 0)
+        v5_take(0, 0, 1, 3)
+        v5_add(0, 0, 1, 2)
+        v5(0, 0, 1, 1)
+        v5(0, 0, 3, 1)
+        flip(1, 1, 1)
+        flip_copy(1, 1, 1)
+        slot_quant(1, 1)
+        flip(1, 0, 1)
+        rm_again()
+        mm(0, 0, 0, 1)
+        mm(0, 0, 1, 0)
+        mm(0, 0, 3, 2)
+        flip_copy(1, 0, 1)
+        slot_quant(1, 0)
+        mm(0, 1, 1, 3)
+        mm(0, 1, 1, 2)
+        v5(0, 0, 1, 0)
         ilv(key_raw, 0, 0, "S")
+        rk_again(1)
+        v5_take(0, 1, 1, 3)
+        v5_add(0, 0, 1, 3)
+        v5_take(0, 1, 1, 2)
+        v5_term(0, 1, 1, 3)
+        mm(0, 0, 3, 3)
+        v5(0, 0, 0, 1)
+        v5(0, 0, 3, 2)
+        v5_add(0, 1, 1, 3)
+        v5(0, 0, 3, 3)
+        mm(0, 1, 2, 1)
+        mm(0, 1, 0, 0)
+        mm(0, 1, 0, 1)
+        v5(0, 1, 2, 1)
+        v5(0, 1, 0, 0)
+        v5(0, 1, 0, 1)
+        tok_ilv(1, 0, "S")
+        mm(0, 0, 2, 2)
+        v5(0, 0, 2, 2)
+        mm(0, 1, 3, 2)
+        v5(0, 1, 3, 2)
+        mm(0, 1, 3, 3)
+        v5(0, 1, 3, 3)
+        ilv(key_raw, 0, 1, "S")
+        mm(0, 0, 2, 1)
+        v5(0, 0, 2, 1)
+        mm(0, 1, 2, 2)
+        mm(0, 1, 3, 1)
+        v5_term(0, 1, 1, 2)
+        v5_add(0, 1, 1, 2)
+        v5_take(0, 1, 2, 2)
+        mm(0, 1, 2, 3)
+        v5_take(0, 1, 2, 3)
+        tok_quant(1, 0)
+        tok_ilv(1, 1, "S")
+        quant("key", 0, 1)
+        v5_term(0, 1, 2, 3)
+        mm(0, 1, 2, 0)
         quant("key", 0, 0)
-        v5(1, 1, 0, 1)
-        mm(1, 1, 3, 0)
-        mm(1, 1, 0, 0)
-        mm(1, 1, 2, 1)
-        v5(1, 1, 3, 1)
-        v5(1, 1, 3, 0)
-        v5(1, 1, 0, 0)
-        mm(1, 1, 2, 0)
-        v5(1, 1, 2, 1)
-        v5(1, 1, 2, 0)
-        v5_take(1, 1, 3, 3)
-        mm(1, 1, 1, 0)
-        v5_term(1, 1, 3, 2)
-        mm(1, 0, 2, 0)
-        v5_term(1, 1, 3, 3)
-        store(0, 0, 0, 1)
-        v5(1, 0, 2, 0)
+        mm(0, 1, 3, 0)
+        mm(0, 1, 1, 0)
+        v5(0, 1, 2, 0)
+        v5_term(0, 1, 2, 2)
+        v5_add(0, 1, 2, 2)
         mm(1, 0, 2, 1)
-        v5(1, 0, 2, 1)
-        store(0, 0, 2, 0)
-        v5(1, 1, 1, 0)
-        mm(1, 1, 1, 1)
-        store(0, 0, 3, 0)
-        mm(1, 0, 3, 1)
-        v5_take(1, 1, 3, 2)
-        v5(1, 1, 1, 1)
-        mm(1, 0, 3, 0)
-        v5_add(1, 1, 3, 2)
-        mm(1, 0, 0, 1)
-        store(0, 0, 1, 1)
-        store(0, 0, 2, 1)
-        v5(1, 0, 3, 0)
-        mm(1, 0, 1, 0)
-        v5(1, 0, 3, 1)
-        v5_add(1, 1, 3, 3)
-        store(0, 0, 3, 1)
-        store(0, 0, 1, 0)
-        store(0, 1, 2, 1)
-        store(0, 1, 0, 0)
-        store(0, 1, 1, 1)
+        v5_take(1, 0, 2, 1)
+        mm(0, 1, 1, 1)
+        v5(0, 1, 1, 0)
+        v5(0, 1, 3, 1)
+        v5(0, 1, 3, 0)
+        tok_quant(1, 1)
+        store(0, 0, 0, 1)
+        v5(0, 1, 1, 1)
+        mm(1, 0, 2, 0)
         mm(1, 0, 0, 0)
-        store(0, 1, 0, 1)
-        v5(1, 0, 0, 1)
-        store(1, 0, 2, 1)
-        store(0, 1, 2, 0)
         v5(1, 0, 0, 0)
-        store(1, 0, 3, 1)
-        store(1, 0, 0, 1)
-        store(1, 1, 2, 1)
+        mm(0, 1, 0, 3)
+        v5(0, 1, 0, 3)
+        mm(0, 1, 0, 2)
+        mm(1, 1, 2, 1)
+        v5(1, 1, 2, 1)
+        mm(1, 1, 2, 0)
+        v5(1, 1, 2, 0)
+        mm(1, 1, 0, 0)
+        mm(1, 0, 0, 1)
+        v5(1, 0, 0, 1)
+        mm(1, 1, 3, 1)
+        v5(0, 1, 0, 2)
+        v5_take(1, 0, 2, 0)
+        v5(1, 1, 3, 1)
+        mm(1, 1, 3, 0)
+        v5(1, 1, 3, 0)
+        ilv(key_raw, 0, 3, "S")
+        mm(1, 0, 1, 0)
+        ilv(key_raw, 1, 3, "S")
+        quant("key", 0, 3)
+        mm(1, 1, 0, 1)
+        v5_take(1, 1, 0, 0)
+        mm(1, 1, 1, 1)
+        quant("key", 1, 3)
+        store(0, 0, 1, 1)
+        mm(1, 0, 3, 1)
+        v5(1, 0, 3, 1)
+        mm(1, 0, 3, 0)
+        v5(1, 0, 3, 0)
+        v5(1, 0, 1, 0)
+        mm(1, 1, 1, 3)
+        v5_take(1, 1, 0, 1)
+        mm(1, 0, 1, 1)
+        v5_add(0, 1, 2, 3)
+        v5(1, 0, 1, 1)
+        mm(1, 1, 0, 3)
+        v5(1, 1, 1, 1)
+        ilv(key_raw, 1, 2, "S")
+        mm(1, 1, 1, 0)
+        quant("key", 1, 2)
+        v5(1, 1, 1, 0)
+        mm(1, 1, 3, 3)
+        v5_term(1, 0, 2, 0)
+        v5_add(1, 0, 2, 0)
+        v5_term(1, 0, 2, 1)
+        v5_add(1, 0, 2, 1)
+        store(0, 0, 3, 0)
+        mm(1, 0, 0, 3)
+        ilv(key_raw, 0, 2, "S")
+        quant("key", 0, 2)
+        mm(1, 1, 3, 2)
+        mm(1, 1, 1, 2)
+        store(0, 0, 1, 0)
+        v5(1, 1, 3, 3)
+        mm(1, 0, 0, 2)
+        v5(1, 1, 3, 2)
+        v5_term(1, 1, 1, 3)
+        mm(1, 0, 1, 2)
+        mm(1, 0, 2, 2)
+        store(0, 0, 0, 0)
+        v5(1, 0, 0, 3)
+        v5_take(1, 1, 1, 3)
+        mm(1, 1, 0, 2)
+        v5(1, 0, 0, 2)
+        store(0, 0, 3, 1)
+        store(0, 1, 1, 1)
+        store(0, 1, 0, 0)
+        store(0, 0, 2, 1)
+        v5_take(1, 1, 1, 2)
+        v5(1, 1, 0, 3)
         store(0, 1, 3, 1)
-        store(1, 0, 1, 1)
+        mm(1, 0, 1, 3)
+        store(0, 0, 2, 0)
+        mm(1, 0, 2, 3)
+        store(0, 1, 2, 0)
+        mm(1, 1, 2, 2)
+        store(0, 1, 2, 1)
+        mm(1, 0, 3, 2)
         store(0, 1, 3, 0)
         store(0, 1, 1, 0)
-        store(1, 1, 0, 1)
-        store(1, 1, 1, 1)
-        mm(1, 0, 1, 1)
-        store(1, 1, 3, 1)
-        store(1, 1, 3, 0)
-        store(1, 1, 0, 0)
-        v5(1, 0, 1, 0)
-        store(1, 1, 2, 0)
+        v5_term(1, 1, 0, 1)
+        v5_add(1, 1, 0, 1)
         store(1, 0, 2, 0)
-        v5(1, 0, 1, 1)
-        store(1, 1, 1, 0)
-        store(1, 0, 3, 0)
+        store(1, 1, 2, 0)
+        v5(1, 0, 2, 2)
+        mm(1, 1, 2, 3)
+        store(0, 1, 0, 1)
         store(1, 0, 0, 0)
+        mm(1, 0, 3, 3)
+        v5(1, 1, 0, 2)
+        store(1, 1, 3, 0)
+        v5_term(1, 1, 0, 0)
+        v5(1, 0, 1, 2)
+        v5(1, 0, 1, 3)
+        store(1, 0, 3, 0)
         store(1, 0, 1, 0)
+        v5_add(1, 1, 0, 0)
+        v5(1, 0, 2, 3)
+        v5(1, 1, 2, 2)
+        store(1, 1, 0, 0)
+        store(1, 1, 1, 0)
+        v5(1, 0, 3, 2)
+        v5_term(1, 1, 1, 2)
+        v5_add(1, 1, 1, 2)
+        store(1, 1, 3, 1)
+        v5_add(1, 1, 1, 3)
+        store(1, 0, 0, 1)
+        store(1, 1, 1, 1)
+        store(1, 1, 0, 1)
+        store(1, 0, 1, 1)
+        store(1, 0, 2, 1)
+        v5(1, 1, 2, 3)
+        store(1, 1, 2, 1)
+        v5(1, 0, 3, 3)
+        store(1, 0, 3, 1)

from contextlib import ExitStack

import concourse.mybir as mybir
from concourse.masks import make_identity

P = 128
J = 4
G = 2
N = 1024
D = 2048
DC = 512
FLOPS = 4 * 1024 * 1024 * 2048

F32 = mybir.dt.float32
BF16 = mybir.dt.bfloat16
U32 = mybir.dt.uint32
U8 = mybir.dt.uint8
E4M3 = mybir.dt.float8_e4m3fn_x4
E5M2 = mybir.dt.float8_e5m2_x4
MULT = mybir.AluOpType.mult
ADD = mybir.AluOpType.add
SUB = mybir.AluOpType.subtract
COPY = mybir.ActivationFunctionType.Copy
SQUARE = mybir.ActivationFunctionType.Square


def tile_memory_pa_v_kernel(tc, memory, key, strength, sharpen, sim, w, grad_out, out_0, out_1):
    nc = tc.nc
    mem_hbm = memory.rearrange("(g p j) c h w -> p g j (c h w)", p=P, j=J)
    key_hbm = key.rearrange("(g p j) d -> p g j d", p=P, j=J)
    w_hbm = w.rearrange("(g p j) n -> p g j n", p=P, j=J)
    sim_hbm = sim.rearrange("(g p j) n -> p g j n", p=P, j=J)
    go_hbm = grad_out.rearrange("(g p j) n -> p g j n", p=P, j=J)
    out_0_hbm = out_0.rearrange("(g p j) d -> p g j d", p=P, j=J)
    out_1_hbm = out_1.rearrange("(g p j) c h w -> p g j (c h w)", p=P, j=J)

    with ExitStack() as ctx:
        keep = ctx.enter_context(tc.tile_pool(name="keep", bufs=1))
        rows = ctx.enter_context(tc.tile_pool(name="rows", bufs=8))
        psum = ctx.enter_context(tc.psum_pool(name="psum", bufs=5))

        mem_raw = keep.tile([P, G, J, D], BF16, name="mem_raw")
        key_raw = keep.tile([P, G, J, D], BF16, name="key_raw")
        mem_codes = keep.tile([P, G, D], U32, name="mem_codes", align_bytes=64)
        mem_scales = keep.tile([P, G, D], U8, name="mem_scales", align_bytes=64)
        key_codes = keep.tile([P, G, D], U32, name="key_codes", align_bytes=64)
        key_scales = keep.tile([P, G, D], U8, name="key_scales", align_bytes=64)
        tok_codes = keep.tile([P, G, N], U32, name="tok_codes", align_bytes=64)
        tok_scales = keep.tile([P, G, N], U8, name="tok_scales", align_bytes=64)
        slot_codes = keep.tile([P, G, N], U32, name="slot_codes", align_bytes=64)
        slot_scales = keep.tile([P, G, N], U8, name="slot_scales", align_bytes=64)
        squares = keep.tile([P, D], BF16, name="squares")
        minv_row = keep.tile([P, N], F32, name="minv_row")
        ident = keep.tile([P, P], F32, name="ident")
        ones = keep.tile([P, 1], F32, name="ones")
        half = keep.tile([P, 8], F32, name="half")
        strength_sb = keep.tile([P, G, J], BF16, name="strength_sb")
        sharpen_sb = keep.tile([P, G, J], BF16, name="sharpen_sb")
        fac = keep.tile([P, 8], F32, name="fac")
        mem_ss = keep.tile([P, 8], F32, name="mem_ss")
        key_ss = keep.tile([P, 8], F32, name="key_ss")
        mem_inv = keep.tile([P, 8], F32, name="mem_inv")
        key_inv = keep.tile([P, 8], F32, name="key_inv")
        neg_c = keep.tile([P, 8], F32, name="neg_c")
        row_sum = keep.tile([P, 8], F32, name="row_sum")
        scl = keep.tile([P, 8], F32, name="scl")
        neg_rk = keep.tile([P, 8], F32, name="neg_rk")
        neg_rm = keep.tile([P, 8], F32, name="neg_rm")
        col_sum = keep.tile([P, 8], F32, name="col_sum")

        w_sb, sim_sb, go_sb, wg_sb, dd_sb, grp, go_pairs, spread_ps, flip_ps, terms = {}, {}, {}, {}, {}, {}, {}, {}, {}, {}

        def grouped_tile(eng):
            if eng == "V":
                t = rows.tile([P, DC, J], BF16, name="grouped_v", bufs=2, align_bytes=64)
            else:
                t = rows.tile([P, DC, J], BF16, name="grouped_s", bufs=3, align_bytes=64)
            return t

        def load_w(g, j):
            w_sb[g, j] = rows.tile([P, N], F32, name="w_row")
            nc.sync.dma_start(out=w_sb[g, j][:], in_=w_hbm[:, g, j, :])

        def load_go(g, j, count):
            if (g, j // 2) not in go_pairs:
                go_pairs[g, j // 2] = rows.tile([P, 2, N], BF16, name="go_pair", bufs=2)
            for i in range(j, j + count):
                go_sb[g, i] = go_pairs[g, j // 2][:, i % 2, :]
            nc.sync.dma_start(out=go_pairs[g, j // 2][:, j % 2 : j % 2 + count, :], in_=go_hbm[:, g, j : j + count, :])

        def load_sim(g, j):
            sim_sb[g, j] = rows.tile([P, N], F32, name="sim_row", bufs=4)
            nc.sync.dma_start(out=sim_sb[g, j][:], in_=sim_hbm[:, g, j, :])

        def load_mem(g, j, count):
            nc.sync.dma_start(out=mem_raw[:, g, j : j + count, :], in_=mem_hbm[:, g, j : j + count, :])

        def load_key(g, j, count):
            nc.sync.dma_start(out=key_raw[:, g, j : j + count, :], in_=key_hbm[:, g, j : j + count, :])

        def norm(raw, ss, g, j):
            col = 4 * g + j
            nc.scalar.activation(out=squares[:], in_=raw[:, g, j, :], func=SQUARE, accum_out=ss[:, col : col + 1])

        def floor_ss(ss, g):
            cols = slice(4 * g, 4 * g + 4)
            nc.vector.tensor_scalar(out=ss[:, cols], in0=ss[:, cols], scalar1=1e-16, scalar2=None, op0=mybir.AluOpType.max)

        def inverse_root(ss, inv, g):
            cols = slice(4 * g, 4 * g + 4)
            nc.gpsimd.tensor_tensor(out=inv[:, cols], in0=ss[:, cols], in1=half[:, cols], op=mybir.AluOpType.pow)

        def spread(g):
            spread_ps[g] = psum.tile([P, J, P], F32, name="flip", bufs=2)
            for j in range(J):
                col = 4 * g + j
                nc.tensor.transpose(spread_ps[g][:, j, :], mem_inv[:, col : col + 1].to_broadcast([P, P]), ident[:])

        def keep_minv(g):
            nc.vector.tensor_copy(
                out=minv_row[:, 512 * g : 512 * (g + 1)].rearrange("p (m j) -> p m j", j=J), in_=spread_ps[g][:].rearrange("p j m -> p m j")
            )

        def v1(g, j):
            col = 4 * g + j
            wg_sb[g, j] = rows.tile([P, N], F32, name="wg_row", bufs=2)
            nc.vector.scalar_tensor_tensor(
                out=wg_sb[g, j][:], in0=w_sb[g, j][:], scalar=-1.0, in1=go_sb[g, j][:], op0=MULT, op1=MULT, accum_out=neg_c[:, col : col + 1]
            )

        def v2(g, j):
            col = 4 * g + j
            nc.vector.scalar_tensor_tensor(
                out=w_sb[g, j][:], in0=w_sb[g, j][:], scalar=neg_c[:, col : col + 1], in1=wg_sb[g, j][:], op0=MULT, op1=SUB
            )

        def v3(g, j):
            col = 4 * g + j
            nc.vector.scalar_tensor_tensor(
                out=sim_sb[g, j][:], in0=w_sb[g, j][:], scalar=fac[:, col : col + 1], in1=sim_sb[g, j][:], op0=MULT, op1=MULT,
                accum_out=row_sum[:, col : col + 1],
            )

        def colsum(g, j):
            for blk in range(8):
                q, t = divmod(blk, J)
                nc.tensor.matmul(
                    sums[:, blk, 4 * g + j : 4 * g + j + 1], lhsT=sim_sb[g, j][:, 512 * q + t : 512 * (q + 1) : J], rhs=ones[:], start=True, stop=True
                )

        def scales_of_group(g):
            cols = slice(4 * g, 4 * g + 4)
            nc.vector.tensor_mul(scl[:, cols], fac[:, cols], key_inv[:, cols])

        def rk_of_group(g):
            cols = slice(4 * g, 4 * g + 4)
            nc.vector.scalar_tensor_tensor(out=neg_rk[:, cols], in0=row_sum[:, cols], scalar=-1.0, in1=key_inv[:, cols], op0=MULT, op1=MULT)

        def rk_again(g):
            cols = slice(4 * g, 4 * g + 4)
            nc.vector.tensor_mul(neg_rk[:, cols], neg_rk[:, cols], key_inv[:, cols])

        def rm_sum():
            nc.vector.tensor_reduce(out=col_sum[:], in_=sums[:], axis=mybir.AxisListType.X, op=ADD)

        def rm_of_all():
            nc.vector.scalar_tensor_tensor(out=neg_rm[:], in0=col_sum[:], scalar=-1.0, in1=mem_inv[:], op0=MULT, op1=MULT)

        def rm_again():
            nc.vector.tensor_mul(neg_rm[:], neg_rm[:], mem_inv[:])

        def v4(g, j):
            col = 4 * g + j
            if g not in dd_sb:
                dd_sb[g] = rows.tile([P, J, N], BF16, name="dd", bufs=1)
            nc.vector.scalar_tensor_tensor(
                out=dd_sb[g][:, j, :], in0=w_sb[g, j][:], scalar=scl[:, col : col + 1], in1=minv_row[:], op0=MULT, op1=MULT
            )

        def ilv(raw, g, dc, eng):
            t = grouped_tile(eng)
            grp["mem" if raw is mem_raw else "key", g, dc] = t
            out = t[:].rearrange("p (c i) j -> p c j i", i=4)
            in_ = raw[:, g, :, dc * DC : (dc + 1) * DC].rearrange("p j (c i) -> p c j i", i=4)
            if eng == "S":
                nc.scalar.copy(out=out, in_=in_)
            elif eng == "V":
                nc.vector.tensor_copy(out=out, in_=in_)
            else:
                for s in range(4):
                    nc.gpsimd.tensor_scalar(
                        out=out[:, 32 * s : 32 * (s + 1)], in0=in_[:, 32 * s : 32 * (s + 1)], scalar1=1.0, scalar2=0.0, op0=MULT, op1=ADD
                    )

        def quant(name, g, dc):
            codes, scales = (mem_codes, mem_scales) if name == "mem" else (key_codes, key_scales)
            cols = slice(dc * DC, (dc + 1) * DC)
            t = grp[name, g, dc]
            nc.vector.quantize_mx(out=codes[:, g, cols].bitcast(E4M3), scales=scales[:, g, cols], in_=t[:].rearrange("p c j -> p (c j)"))

        def tok_ilv(g, q, eng):
            t = grouped_tile(eng)
            grp["tok", g, q] = t
            out = t[:].rearrange("p (t m) j -> p t m j", t=J)
            in_ = dd_sb[g][:, :, 512 * q : 512 * (q + 1)].rearrange("p j (m t) -> p t m j", t=J)
            if eng == "V":
                nc.vector.tensor_copy(out=out, in_=in_)
            else:
                nc.scalar.copy(out=out, in_=in_)

        def tok_quant(g, q):
            cols = slice(512 * q, 512 * (q + 1))
            t = grp["tok", g, q]
            nc.vector.quantize_mx(out=tok_codes[:, g, cols].bitcast(E5M2), scales=tok_scales[:, g, cols], in_=t[:].rearrange("p c j -> p (c j)"))

        def flip(g, q, jj):
            words = dd_sb[g][:].rearrange("p j n -> p (j n)").bitcast(F32)
            bank = psum.tile([P, 2, 2, P], F32, name="flip", bufs=2)
            flip_ps[g, q, jj] = bank
            for e in range(2):
                for v in range(2):
                    first = 512 * (2 * jj + e) + 256 * q + v
                    nc.tensor.transpose(bank[:, e, v, :], words[:, first : first + 255 : 2], ident[:])

        def flip_copy(g, q, jj):
            if ("slot", g, q) not in grp:
                grp["slot", g, q] = grouped_tile("S")
            t_words = grp["slot", g, q][:].rearrange("p c t -> p (c t)").bitcast(F32)
            nc.scalar.copy(
                out=t_words[:, 512 * jj : 512 * (jj + 1)].rearrange("p (e b v) -> p e b v", e=2, v=2),
                in_=flip_ps[g, q, jj][:].rearrange("p e v b -> p e b v"),
            )

        def slot_quant(g, q):
            cols = slice(512 * g, 512 * (g + 1))
            t = grp["slot", g, q]
            nc.vector.quantize_mx(out=slot_codes[:, q, cols].bitcast(E5M2), scales=slot_scales[:, q, cols], in_=t[:].rearrange("p c t -> p (c t)"))

        accs = {}

        def mm(o, g, j, dc):
            acc = psum.tile([P, DC], F32, name="acc")
            accs[o, g, j, dc] = acc
            first = 512 * g + 128 * j
            for q in range(G):
                if o == 0:
                    lc, ls, rc, rs = slot_codes[:, q, first : first + P], slot_scales[:, q, first : first + P], mem_codes, mem_scales
                else:
                    lc, ls, rc, rs = tok_codes[:, q, first : first + P], tok_scales[:, q, first : first + P], key_codes, key_scales
                cols = slice(dc * DC, (dc + 1) * DC)
                nc.tensor.matmul_mx(
                    acc[:], lhsT=lc.bitcast(E5M2), lhsT_scale=ls, rhs=rc[:, q, cols].bitcast(E4M3), rhs_scale=rs[:, q, cols], start=(q == 0), stop=(q == G - 1)
                )

        stage = {}

        def half_stage(o, g, j, dc, eng):
            if (o, g, j, dc // 2) not in stage:
                if eng == "V":
                    stage[o, g, j, dc // 2] = rows.tile([P, N], F32, name="w_row")
                else:
                    stage[o, g, j, dc // 2] = rows.tile([P, N], F32, name="stage_s", bufs=2)
            h = dc % 2
            return stage[o, g, j, dc // 2][:, h * DC : (h + 1) * DC]

        def subtrahend(o, g, j, dc):
            col = 4 * g + j
            raw, neg = (key_raw, neg_rk) if o == 0 else (mem_raw, neg_rm)
            return raw[:, g, j, dc * DC : (dc + 1) * DC], neg[:, col : col + 1]

        def v5(o, g, j, dc):
            r, n = subtrahend(o, g, j, dc)
            nc.vector.scalar_tensor_tensor(out=half_stage(o, g, j, dc, "V"), in0=r, scalar=n, in1=accs[o, g, j, dc][:], op0=MULT, op1=ADD)

        def v5_take(o, g, j, dc):
            nc.scalar.copy(out=half_stage(o, g, j, dc, "S"), in_=accs[o, g, j, dc][:])

        def v5_term(o, g, j, dc):
            r, n = subtrahend(o, g, j, dc)
            terms[o, g, j, dc] = rows.tile([P, DC], F32, name="term", bufs=2)
            nc.gpsimd.tensor_scalar(out=terms[o, g, j, dc][:], in0=r, scalar1=n, scalar2=0.0, op0=MULT, op1=ADD)

        def v5_add(o, g, j, dc):
            out = half_stage(o, g, j, dc, "S")
            nc.gpsimd.tensor_tensor(out=out, in0=out, in1=terms[o, g, j, dc][:], op=ADD)

        def store(o, g, j, h):
            hbm = out_0_hbm if o == 0 else out_1_hbm
            nc.sync.dma_start(out=hbm[:, g, j, 2 * h * DC : 2 * (h + 1) * DC], in_=stage[o, g, j, h][:])

        sums = psum.tile([P, 8, 8], F32, name="sums", bufs=1)
        ctx.enter_context(tc.manual_schedule())
        load_mem(1, 0, 2)
        norm(mem_raw, mem_ss, 1, 1)
        nc.vector.memset(half[:], -0.5)
        load_mem(1, 2, 2)
        ilv(mem_raw, 1, 1, "V")
        ilv(mem_raw, 1, 3, "V")
        ilv(mem_raw, 1, 2, "S")
        quant("mem", 1, 2)
        quant("mem", 1, 3)
        load_mem(0, 2, 2)
        norm(mem_raw, mem_ss, 0, 3)
        load_mem(0, 1, 1)
        quant("mem", 1, 1)
        norm(mem_raw, mem_ss, 1, 0)
        load_mem(0, 0, 1)
        norm(mem_raw, mem_ss, 1, 3)
        ilv(mem_raw, 0, 3, "V")
        nc.sync.dma_start(out=sharpen_sb[:], in_=sharpen.rearrange("(g p j) o -> p g (j o)", p=P, j=J))
        make_identity(nc, ident[:])
        nc.sync.dma_start(out=strength_sb[:], in_=strength.rearrange("(g p j) o -> p g (j o)", p=P, j=J))
        load_go(0, 2, 2)
        load_w(0, 2)
        load_w(0, 3)
        nc.vector.tensor_mul(fac[:], strength_sb[:].rearrange("p g j -> p (g j)"), sharpen_sb[:].rearrange("p g j -> p (g j)"))
        load_sim(0, 3)
        ilv(mem_raw, 0, 1, "V")
        v1(0, 2)
        v1(0, 3)
        v2(0, 2)
        v2(0, 3)
        load_sim(0, 2)
        load_w(0, 1)
        load_go(0, 1, 1)
        v1(0, 1)
        quant("mem", 0, 3)
        nc.vector.memset(ones[:], 1.0)
        norm(mem_raw, mem_ss, 0, 0)
        v3(0, 3)
        v2(0, 1)
        norm(mem_raw, mem_ss, 1, 2)
        v3(0, 2)
        load_w(1, 0)
        load_sim(0, 1)
        v3(0, 1)
        load_go(0, 0, 1)
        load_w(0, 0)
        v1(0, 0)
        load_key(0, 2, 2)
        colsum(0, 3)
        colsum(0, 2)
        norm(mem_raw, mem_ss, 0, 2)
        norm(mem_raw, mem_ss, 0, 1)
        floor_ss(mem_ss, 0)
        inverse_root(mem_ss, mem_inv, 0)
        floor_ss(mem_ss, 1)
        spread(0)
        norm(key_raw, key_ss, 0, 2)
        inverse_root(mem_ss, mem_inv, 1)
        spread(1)
        quant("mem", 0, 1)
        norm(key_raw, key_ss, 0, 3)
        v2(0, 0)
        load_sim(0, 0)
        v3(0, 0)
        load_go(1, 0, 2)
        colsum(0, 0)
        v1(1, 0)
        load_key(0, 0, 2)
        norm(key_raw, key_ss, 0, 0)
        keep_minv(0)
        load_w(1, 1)
        load_w(1, 2)
        v1(1, 1)
        v2(1, 0)
        norm(key_raw, key_ss, 0, 1)
        floor_ss(key_ss, 0)
        keep_minv(1)
        inverse_root(key_ss, key_inv, 0)
        load_sim(1, 0)
        scales_of_group(0)
        colsum(0, 1)
        rk_of_group(0)
        rk_again(0)
        v4(0, 3)
        load_key(1, 2, 2)
        load_go(1, 2, 2)
        v4(0, 2)
        flip(0, 0, 1)
        v4(0, 1)
        v4(0, 0)
        ilv(mem_raw, 0, 2, "S")
        norm(key_raw, key_ss, 1, 2)
        v2(1, 1)
        quant("mem", 0, 2)
        v5_term(0, 0, 1, 2)
        load_key(1, 0, 2)
        flip_copy(0, 0, 1)
        flip(0, 1, 1)
        flip_copy(0, 1, 1)
        load_sim(1, 1)
        norm(key_raw, key_ss, 1, 0)
        v3(1, 1)
        flip(0, 1, 0)
        flip_copy(0, 1, 0)
        flip(0, 0, 0)
        load_w(1, 3)
        v1(1, 3)
        slot_quant(0, 1)
        flip_copy(0, 0, 0)
        colsum(1, 1)
        slot_quant(0, 0)
        mm(0, 0, 0, 3)
        v1(1, 2)
        v5_term(0, 0, 1, 3)
        mm(0, 0, 0, 2)
        mm(0, 0, 1, 2)
        mm(0, 0, 2, 3)
        mm(0, 0, 3, 1)
        ilv(mem_raw, 1, 0, "S")
        v5(0, 0, 0, 3)
        v5(0, 0, 0, 2)
        ilv(mem_raw, 0, 0, "S")
        v2(1, 2)
        quant("mem", 0, 0)
        load_sim(1, 2)
        norm(key_raw, key_ss, 1, 3)
        quant("mem", 1, 0)
        v3(1, 2)
        colsum(1, 2)
        mm(0, 0, 1, 1)
        v2(1, 3)
        mm(0, 0, 2, 0)
        v3(1, 0)
        v5(0, 0, 2, 3)
        norm(key_raw, key_ss, 1, 1)
        floor_ss(key_ss, 1)
        load_sim(1, 3)
        v3(1, 3)
        mm(0, 0, 3, 0)
        v5(0, 0, 3, 0)
        inverse_root(key_ss, key_inv, 1)
        scales_of_group(1)
        tok_ilv(0, 0, "S")
        tok_quant(0, 0)
        colsum(1, 3)
        rk_of_group(1)
        v5(0, 0, 2, 0)
        v4(1, 1)
        v4(1, 0)
        tok_ilv(0, 1, "S")
        tok_quant(0, 1)
        ilv(key_raw, 1, 0, "S")
        v4(1, 2)
        colsum(1, 0)
        quant("key", 1, 0)
        rm_sum()
        flip(1, 0, 0)
        v4(1, 3)
        ilv(key_raw, 1, 1, "S")
        quant("key", 1, 1)
        flip(1, 1, 0)
        flip_copy(1, 0, 0)
        v5_take(0, 0, 1, 2)
        flip_copy(1, 1, 0)
        mm(0, 0, 0, 0)
        rm_of_all()
        mm(0, 0, 1, 3)
        v5(0, 0, 0, 0)
        v5_take(0, 0, 1, 3)
        v5_add(0, 0, 1, 2)
        v5(0, 0, 1, 1)
        v5(0, 0, 3, 1)
        flip(1, 1, 1)
        flip_copy(1, 1, 1)
        slot_quant(1, 1)
        flip(1, 0, 1)
        rm_again()
        mm(0, 0, 0, 1)
        mm(0, 0, 1, 0)
        mm(0, 0, 3, 2)
        flip_copy(1, 0, 1)
        slot_quant(1, 0)
        mm(0, 1, 1, 3)
        mm(0, 1, 1, 2)
        v5(0, 0, 1, 0)
        ilv(key_raw, 0, 0, "S")
        rk_again(1)
        v5_take(0, 1, 1, 3)
        v5_add(0, 0, 1, 3)
        v5_take(0, 1, 1, 2)
        v5_term(0, 1, 1, 3)
        mm(0, 0, 3, 3)
        v5(0, 0, 0, 1)
        v5(0, 0, 3, 2)
        v5_add(0, 1, 1, 3)
        v5(0, 0, 3, 3)
        mm(0, 1, 2, 1)
        mm(0, 1, 0, 0)
        mm(0, 1, 0, 1)
        v5(0, 1, 2, 1)
        v5(0, 1, 0, 0)
        v5(0, 1, 0, 1)
        tok_ilv(1, 0, "S")
        mm(0, 0, 2, 2)
        v5(0, 0, 2, 2)
        mm(0, 1, 3, 2)
        v5(0, 1, 3, 2)
        mm(0, 1, 3, 3)
        v5(0, 1, 3, 3)
        ilv(key_raw, 0, 1, "S")
        mm(0, 0, 2, 1)
        v5(0, 0, 2, 1)
        mm(0, 1, 2, 2)
        mm(0, 1, 3, 1)
        v5_term(0, 1, 1, 2)
        v5_add(0, 1, 1, 2)
        v5_take(0, 1, 2, 2)
        mm(0, 1, 2, 3)
        v5_take(0, 1, 2, 3)
        tok_quant(1, 0)
        tok_ilv(1, 1, "S")
        quant("key", 0, 1)
        v5_term(0, 1, 2, 3)
        mm(0, 1, 2, 0)
        quant("key", 0, 0)
        mm(0, 1, 3, 0)
        mm(0, 1, 1, 0)
        v5(0, 1, 2, 0)
        v5_term(0, 1, 2, 2)
        v5_add(0, 1, 2, 2)
        mm(1, 0, 2, 1)
        v5_take(1, 0, 2, 1)
        mm(0, 1, 1, 1)
        v5(0, 1, 1, 0)
        v5(0, 1, 3, 1)
        v5(0, 1, 3, 0)
        tok_quant(1, 1)
        store(0, 0, 0, 1)
        v5(0, 1, 1, 1)
        mm(1, 0, 2, 0)
        mm(1, 0, 0, 0)
        v5(1, 0, 0, 0)
        mm(0, 1, 0, 3)
        v5(0, 1, 0, 3)
        mm(0, 1, 0, 2)
        mm(1, 1, 2, 1)
        v5(1, 1, 2, 1)
        mm(1, 1, 2, 0)
        v5(1, 1, 2, 0)
        mm(1, 1, 0, 0)
        mm(1, 0, 0, 1)
        v5(1, 0, 0, 1)
        mm(1, 1, 3, 1)
        v5(0, 1, 0, 2)
        v5_take(1, 0, 2, 0)
        v5(1, 1, 3, 1)
        mm(1, 1, 3, 0)
        v5(1, 1, 3, 0)
        ilv(key_raw, 0, 3, "S")
        mm(1, 0, 1, 0)
        ilv(key_raw, 1, 3, "S")
        quant("key", 0, 3)
        mm(1, 1, 0, 1)
        v5_take(1, 1, 0, 0)
        mm(1, 1, 1, 1)
        quant("key", 1, 3)
        store(0, 0, 1, 1)
        mm(1, 0, 3, 1)
        v5(1, 0, 3, 1)
        mm(1, 0, 3, 0)
        v5(1, 0, 3, 0)
        v5(1, 0, 1, 0)
        mm(1, 1, 1, 3)
        v5_take(1, 1, 0, 1)
        mm(1, 0, 1, 1)
        v5_add(0, 1, 2, 3)
        v5(1, 0, 1, 1)
        mm(1, 1, 0, 3)
        v5(1, 1, 1, 1)
        ilv(key_raw, 1, 2, "S")
        mm(1, 1, 1, 0)
        quant("key", 1, 2)
        v5(1, 1, 1, 0)
        mm(1, 1, 3, 3)
        v5_term(1, 0, 2, 0)
        v5_add(1, 0, 2, 0)
        v5_term(1, 0, 2, 1)
        v5_add(1, 0, 2, 1)
        store(0, 0, 3, 0)
        mm(1, 0, 0, 3)
        ilv(key_raw, 0, 2, "S")
        quant("key", 0, 2)
        mm(1, 1, 3, 2)
        mm(1, 1, 1, 2)
        store(0, 0, 1, 0)
        v5(1, 1, 3, 3)
        mm(1, 0, 0, 2)
        v5(1, 1, 3, 2)
        v5_term(1, 1, 1, 3)
        mm(1, 0, 1, 2)
        mm(1, 0, 2, 2)
        store(0, 0, 0, 0)
        v5(1, 0, 0, 3)
        v5_take(1, 1, 1, 3)
        mm(1, 1, 0, 2)
        v5(1, 0, 0, 2)
        store(0, 0, 3, 1)
        store(0, 1, 1, 1)
        store(0, 1, 0, 0)
        store(0, 0, 2, 1)
        v5_take(1, 1, 1, 2)
        v5(1, 1, 0, 3)
        store(0, 1, 3, 1)
        mm(1, 0, 1, 3)
        store(0, 0, 2, 0)
        mm(1, 0, 2, 3)
        store(0, 1, 2, 0)
        mm(1, 1, 2, 2)
        store(0, 1, 2, 1)
        mm(1, 0, 3, 2)
        store(0, 1, 3, 0)
        store(0, 1, 1, 0)
        v5_term(1, 1, 0, 1)
        v5_add(1, 1, 0, 1)
        store(1, 0, 2, 0)
        store(1, 1, 2, 0)
        v5(1, 0, 2, 2)
        mm(1, 1, 2, 3)
        store(0, 1, 0, 1)
        store(1, 0, 0, 0)
        mm(1, 0, 3, 3)
        v5(1, 1, 0, 2)
        store(1, 1, 3, 0)
        v5_term(1, 1, 0, 0)
        v5(1, 0, 1, 2)
        v5(1, 0, 1, 3)
        store(1, 0, 3, 0)
        store(1, 0, 1, 0)
        v5_add(1, 1, 0, 0)
        v5(1, 0, 2, 3)
        v5(1, 1, 2, 2)
        store(1, 1, 0, 0)
        store(1, 1, 1, 0)
        v5(1, 0, 3, 2)
        v5_term(1, 1, 1, 2)
        v5_add(1, 1, 1, 2)
        store(1, 1, 3, 1)
        v5_add(1, 1, 1, 3)
        store(1, 0, 0, 1)
        store(1, 1, 1, 1)
        store(1, 1, 0, 1)
        store(1, 0, 1, 1)
        store(1, 0, 2, 1)
        v5(1, 1, 2, 3)
        store(1, 1, 2, 1)
        v5(1, 0, 3, 3)
        store(1, 0, 3, 1)
